import numpy as np
import ml_dtypes


def mxq(x, axis, fmt="e4m3"):
    dtype, down = {"e4m3": (ml_dtypes.float8_e4m3fn, 7), "e5m2": (ml_dtypes.float8_e5m2, 14)}[fmt]
    v = np.moveaxis(np.asarray(x, np.float32).astype(ml_dtypes.bfloat16).astype(np.float64), axis, -1)
    blocks = v.reshape(v.shape[:-1] + (-1, 32))
    amax = np.abs(blocks).max(-1, keepdims=True)
    byte = np.maximum(np.where(amax > 0, np.frexp(amax)[1] - 1 + 127, 0) - down, 1)
    scale = np.exp2(byte - 127.0)
    codes = (blocks / scale).astype(np.float32).astype(dtype).astype(np.float64)
    return np.moveaxis((codes * scale).reshape(v.shape), -1, axis)


WIDE = False


def mx_kscale(k):
    if not WIDE:
        return np.ones(k)
    levels = np.array([10, -10, 5, -5, 0])
    a = np.random.permutation(np.resize(levels, k // 512 * 4)).reshape(k // 512, 4)
    idx = np.arange(k)
    return np.exp2(a[idx // 512, idx % 128 // 32])


BF16 = ml_dtypes.bfloat16


def bf(x):
    return np.asarray(x, np.float32).astype(BF16)


def f64(x):
    return np.asarray(x).astype(np.float64)


E2M1 = np.array([0.0, 0.5, 1.0, 1.5, 2.0, 3.0, 4.0, 6.0, -0.0, -0.5, -1.0, -1.5, -2.0, -3.0, -4.0, -6.0])


def pack_weight(w, fmt):
    k, n = w.shape
    w = f64(bf(w)).reshape(k // 32, 32, n)
    amax = np.abs(w).max(1)
    if fmt == "e4m3":
        byte = np.frexp(amax)[1] - 1 + 127 - 7
    else:
        mant, ex = np.frexp(amax / 6.0)
        byte = np.where(mant > 0.5, ex, ex - 1) + 127
    byte = np.clip(np.where(amax > 0, byte, 1), 1, 254)
    scaled = (w * np.exp2(127.0 - byte)[:, None, :]).reshape(k, n).astype(np.float32)
    by_word = np.ascontiguousarray(scaled.reshape(k // 512, 128, 4, n).transpose(0, 1, 3, 2))
    if fmt == "e4m3":
        words = by_word.astype(ml_dtypes.float8_e4m3fn).view(np.uint8)
    else:
        c = by_word.astype(ml_dtypes.float4_e2m1fn).view(np.uint8) & 0xF
        words = c[..., 0::2] | (c[..., 1::2] << 4)
    return np.ascontiguousarray(words), np.ascontiguousarray(byte.astype(np.uint8).reshape(k // 512, 16, n))


def unpack_weight(words, scales, fmt):
    g, p, n, _ = words.shape
    if fmt == "e4m3":
        vals = np.ascontiguousarray(words).view(ml_dtypes.float8_e4m3fn).astype(np.float64)
    else:
        nib = np.empty((g, p, n, 4), np.uint8)
        nib[..., 0::2] = words & 0xF
        nib[..., 1::2] = words >> 4
        vals = E2M1[nib]
    vals = vals * np.repeat(np.exp2(scales.astype(np.float64) - 127.0), 8, axis=1)[..., None]
    return vals.transpose(0, 1, 3, 2).reshape(g * 512, n)


B, C, H, W, K, HID, LAT = 4, 512, 16, 16, 8, 512, 32
REDUCTION = -0.1
CLAMP = 500.0
HOT = 1.2 * CLAMP / (-REDUCTION * C * np.sqrt(2.0 / np.pi))


def setup_inputs():
    s = mx_kscale(HID)
    amp = np.where(np.random.random((B, 1, H, W)) < 0.125, HOT, 1.0)
    d = bf(np.tanh(np.random.standard_normal((K, B, HID, H, W))) * s[:, None, None])
    stack = np.random.standard_normal((K, C, HID)) * 1.1 / np.sqrt(HID) / s
    cat = np.ascontiguousarray(np.swapaxes(stack, 1, 2)).reshape(-1, C)
    words, scales = pack_weight(cat, "e4m3")
    x = bf(np.random.standard_normal((B, C, H, W)) * amp)
    return {"d": d, "W_dec_words": words, "W_dec_scales": scales, "x": x}


def reference(d, W_dec_words, W_dec_scales, x):
    xf = f64(x)
    wq = np.swapaxes(unpack_weight(W_dec_words, W_dec_scales, "e4m3").reshape(K, HID, C), 1, 2)
    dq = mxq(f64(d), 2, "e4m3")
    recon = (wq[:, None] @ dq.reshape(K, B, HID, H * W)).reshape(K, B, C, H, W)
    err = np.sum(np.abs(recon - xf[None]), axis=2) * REDUCTION
    logits = np.swapaxes(np.clip(err, -CLAMP, CLAMP), 0, 1)
    e = np.exp(logits - logits.max(axis=1, keepdims=True))
    p = e / e.sum(axis=1, keepdims=True)
    error = np.mean(logits, axis=(2, 3))
    return p, error, np.swapaxes(recon, 0, 1)

@@ -1,0 +1,252 @@
+from contextlib import ExitStack
+
+import concourse.mybir as mybir
+from concourse.masks import make_identity
+
+F32 = mybir.dt.float32
+BF16 = mybir.dt.bfloat16
+I32 = mybir.dt.int32
+U32 = mybir.dt.uint32
+U8 = mybir.dt.uint8
+FP8X4 = mybir.dt.float8_e4m3fn_x4
+ALU = mybir.AluOpType
+ACT = mybir.ActivationFunctionType
+AXIS = mybir.AxisListType
+
+P = 128
+PACK = 4
+CLASSES = 8
+IMAGES = 4
+CHANNELS = 512
+HIDDEN = 512
+PIXELS = 256
+PAIR = 2
+ROUNDS = CLASSES * IMAGES // PAIR
+C_TILES = CHANNELS // P
+PIXEL_TILES = PIXELS // P
+PLANES_PER_TILE = 4
+RUN = 4
+LOADS_AHEAD = 6
+VECTOR_BANKS = 3
+REDUCTION = -0.1
+CLAMP = 500.0
+
+FLOPS = 2 * CLASSES * IMAGES * CHANNELS * HIDDEN * PIXELS
+
+
+def tile_cssrclassifier_pa_e_kernel(tc, d, W_dec_words, W_dec_scales, x, out_0, out_1, out_2):
+    nc = tc.nc
+    with ExitStack() as ctx:
+        ctx.enter_context(tc.manual_schedule())
+        keep = ctx.enter_context(tc.tile_pool(name="keep", bufs=1))
+        raw_pool = ctx.enter_context(tc.tile_pool(name="raw", bufs=LOADS_AHEAD))
+        quant_pool = ctx.enter_context(tc.tile_pool(name="quant", bufs=3))
+        recon_pool = ctx.enter_context(tc.tile_pool(name="recon", bufs=6))
+        unread_pool = ctx.enter_context(tc.tile_pool(name="unread", bufs=4))
+        recon_psum = ctx.enter_context(tc.psum_pool(name="recon_psum", bufs=4))
+        diff_psum = ctx.enter_context(tc.psum_pool(name="diff_psum", bufs=4))
+
+        w_codes = keep.tile([P, CLASSES, CHANNELS], U32, align_bytes=64)
+        w_planes = keep.tile([P, CLASSES // PLANES_PER_TILE, CHANNELS], U8, align_bytes=64)
+        x_raw = keep.tile([P, IMAGES * C_TILES, PIXELS], BF16)
+        neg_x = keep.tile([P, IMAGES * C_TILES, PIXELS], F32)
+        ident = keep.tile([P, P], F32)
+        ones = keep.tile([P, P], F32)
+        prob_cols = keep.tile([P, P], F32)
+        abs_sums = keep.tile([P, IMAGES, PIXEL_TILES, CLASSES], F32)
+        warm = keep.tile([P, 2], F32)
+
+        nc.vector.memset(w_planes[:].bitcast(I32), 0)
+        nc.vector.memset(warm[:], 0.0)
+        nc.scalar.activation(out=warm[:, 1:2], in_=warm[:, 0:1], func=ACT.Exp)
+        make_identity(nc, ident[:])
+        nc.gpsimd.memset(ones[:], 1.0)
+        nc.gpsimd.memset(prob_cols[:], 0.0)
+
+        d_raw = {}
+        d_grouped = {}
+        d_codes = {}
+        d_scales = {}
+        recon_sb = {}
+
+        def load(j):
+            k, pair = divmod(j, IMAGES // PAIR)
+            raw = raw_pool.tile([P, PAIR, PACK * PIXELS], BF16)
+            nc.sync.dma_start(
+                out=raw[:],
+                in_=d[k, PAIR * pair : PAIR * (pair + 1)].rearrange("b (p t) h w -> p b (t h w)", t=PACK),
+            )
+            d_raw[j] = raw
+            if pair != 0:
+                return
+            if k % PLANES_PER_TILE == 0:
+                group = k // PLANES_PER_TILE
+                for quadrant in range(4):
+                    nc.sync.dma_start(
+                        out=w_planes[32 * quadrant : 32 * quadrant + 16, group, :].bitcast(I32),
+                        in_=W_dec_scales[k : k + PLANES_PER_TILE, 4 * quadrant : 4 * quadrant + 4, :].bitcast(I32),
+                    )
+            nc.sync.dma_start(
+                out=w_codes[:, k, :].bitcast(I32),
+                in_=W_dec_words[k].rearrange("p n t -> p (n t)").bitcast(I32),
+            )
+
+        def load_x(pair):
+            rows = slice(PAIR * pair * C_TILES, PAIR * (pair + 1) * C_TILES)
+            nc.sync.dma_start(
+                out=x_raw[:, rows, :],
+                in_=x[PAIR * pair : PAIR * (pair + 1)].rearrange("b (ct p) h w -> p (b ct) (h w)", p=P),
+            )
+
+        def negate_x(pair):
+            for b in range(PAIR * pair, PAIR * (pair + 1)):
+                rows = slice(b * C_TILES, (b + 1) * C_TILES)
+                nc.gpsimd.tensor_scalar(
+                    out=neg_x[:, rows, :], in0=x_raw[:, rows, :], scalar1=-1.0, scalar2=0.0, op0=ALU.mult, op1=ALU.add
+                )
+
+        def regroup(j):
+            grouped = quant_pool.tile([P, PAIR * PIXELS, PACK], BF16, align_bytes=64)
+            to_view = grouped[:].rearrange("p (b c i) t -> p b c t i", b=PAIR, i=RUN)
+            from_view = d_raw[j][:].rearrange("p b (t c i) -> p b c t i", t=PACK, i=RUN)
+            for b2 in range(PAIR):
+                nc.vector.tensor_copy(out=to_view[:, b2], in_=from_view[:, b2])
+            d_grouped[j] = grouped
+
+        def quantise(j):
+            codes = quant_pool.tile([P, PAIR * PIXELS], U32, align_bytes=64)
+            scales = quant_pool.tile([P, PAIR * PIXELS], U8, align_bytes=64)
+            nc.vector.quantize_mx(
+                out=codes[:].bitcast(FP8X4),
+                scales=scales[:],
+                in_=d_grouped[j][:].rearrange("p w t -> p (w t)"),
+            )
+            d_codes[j] = codes
+            d_scales[j] = scales
+
+        def multiply(j):
+            k, pair = divmod(j, IMAGES // PAIR)
+            offset = 4 * (k % PLANES_PER_TILE)
+            group = k // PLANES_PER_TILE
+            recon = recon_pool.tile([P, PAIR, C_TILES, PIXELS], F32)
+            for ct in range(C_TILES):
+                cols = slice(ct * P, (ct + 1) * P)
+                recon_ps = recon_psum.tile([P, PAIR * PIXELS], F32)
+                nc.tensor.matmul_mx(
+                    out=recon_ps[:],
+                    lhsT=w_codes[:, k, cols].bitcast(FP8X4),
+                    lhsT_scale=w_planes[offset:P, group, cols],
+                    rhs=d_codes[j][:].bitcast(FP8X4),
+                    rhs_scale=d_scales[j][:],
+                    start=True,
+                    stop=True,
+                )
+                by_image = recon_ps[:].rearrange("p (b w) -> p b w", b=PAIR)
+                if ct < VECTOR_BANKS:
+                    nc.vector.tensor_copy(out=recon[:, :, ct, :], in_=by_image)
+                else:
+                    nc.scalar.copy(out=recon[:, :, ct, :], in_=by_image)
+            for b2 in range(PAIR):
+                nc.sync.dma_start(
+                    out=out_2[PAIR * pair + b2, k].rearrange("(ct p) h w -> p ct (h w)", p=P),
+                    in_=recon[:, b2, :, :],
+                )
+            recon_sb[j] = recon
+
+        def l1_error(j):
+            k, pair = divmod(j, IMAGES // PAIR)
+            for b2 in range(PAIR):
+                b = PAIR * pair + b2
+                for half in range(PIXEL_TILES):
+                    pixels = slice(half * P, (half + 1) * P)
+                    diff_ps = diff_psum.tile([P, CHANNELS], F32)
+                    for ct in range(C_TILES):
+                        block = diff_ps[:, ct * P : (ct + 1) * P]
+                        nc.tensor.matmul(
+                            out=block, lhsT=neg_x[:, b * C_TILES + ct, pixels], rhs=ident[:],
+                            is_transpose=True, start=True, stop=False,
+                        )
+                        nc.tensor.matmul(
+                            out=block, lhsT=recon_sb[j][:, b2, ct, pixels], rhs=ident[:],
+                            is_transpose=True, start=False, stop=True,
+                        )
+                    unread = unread_pool.tile([P, CHANNELS], BF16)
+                    nc.scalar.activation(
+                        out=unread[:], in_=diff_ps[:], func=ACT.Abs, accum_out=abs_sums[:, b, half, k : k + 1]
+                    )
+
+        load(0)
+        load(1)
+        load_x(0)
+        load(2)
+        load_x(1)
+        for j in range(3, LOADS_AHEAD):
+            load(j)
+        regroup(0)
+        quantise(0)
+        regroup(1)
+        negate_x(0)
+        negate_x(1)
+        for j in range(ROUNDS + 1):
+            if j + LOADS_AHEAD < ROUNDS:
+                load(j + LOADS_AHEAD)
+            if j + 2 < ROUNDS:
+                regroup(j + 2)
+            if j + 1 < ROUNDS:
+                quantise(j + 1)
+            if j < ROUNDS:
+                multiply(j)
+            if j >= 1:
+                l1_error(j - 1)
+
+        logits = keep.tile([P, IMAGES, PIXEL_TILES, CLASSES], F32)
+        nc.vector.tensor_scalar(
+            out=logits[:], in0=abs_sums[:], scalar1=REDUCTION, scalar2=-CLAMP, op0=ALU.mult, op1=ALU.max
+        )
+        nc.vector.tensor_scalar_min(out=logits[:], in0=logits[:], scalar1=CLAMP)
+
+        halves = keep.tile([P, IMAGES, CLASSES], F32)
+        nc.vector.tensor_tensor(out=halves[:], in0=logits[:, :, 0, :], in1=logits[:, :, 1, :], op=ALU.add)
+        mean_ps = diff_psum.tile([P, CHANNELS], F32, tag="diff_ps")
+        nc.tensor.matmul(
+            out=mean_ps[:, 0 : IMAGES * CLASSES], lhsT=ones[:], rhs=halves[:].rearrange("p b k -> p (b k)"),
+            start=True, stop=True,
+        )
+
+        group_shape = [P, IMAGES, PIXEL_TILES, CLASSES]
+        top = keep.tile([P, IMAGES, PIXEL_TILES], F32)
+        nc.vector.tensor_reduce(out=top[:], in_=logits[:], axis=AXIS.X, op=ALU.max)
+        shifted = keep.tile(group_shape, F32)
+        nc.vector.tensor_tensor(
+            out=shifted[:], in0=logits[:], in1=top[:].unsqueeze(3).to_broadcast(group_shape), op=ALU.subtract
+        )
+        expd = keep.tile(group_shape, F32)
+        nc.scalar.activation(out=expd[:], in_=shifted[:], func=ACT.Exp)
+        mean_sb = keep.tile([P, CLASSES], F32)
+        for b in range(IMAGES):
+            nc.scalar.mul(
+                out=mean_sb[32 * b : 32 * b + 1, :],
+                in_=mean_ps[32 * b : 32 * b + 1, b * CLASSES : (b + 1) * CLASSES],
+                mul=1.0 / PIXELS,
+            )
+        nc.sync.dma_start(out=out_1, in_=mean_sb[0:P:32, :])
+        total = keep.tile([P, IMAGES, PIXEL_TILES], F32)
+        nc.vector.tensor_reduce(out=total[:], in_=expd[:], axis=AXIS.X, op=ALU.add)
+        inverse = keep.tile([P, IMAGES, PIXEL_TILES], F32)
+        nc.vector.reciprocal(out=inverse[:], in_=total[:])
+        nc.vector.tensor_tensor(
+            out=prob_cols[:, 0 : IMAGES * CLASSES * PIXEL_TILES].rearrange(
+                "p (b k s) -> p b s k", b=IMAGES, k=CLASSES
+            ),
+            in0=expd[:],
+            in1=inverse[:].unsqueeze(3).to_broadcast(group_shape),
+            op=ALU.mult,
+        )
+        prob_ps = diff_psum.tile([P, CHANNELS], F32, tag="diff_ps")
+        nc.tensor.transpose(out=prob_ps[:, 0:P], in_=prob_cols[:], identity=ident[:])
+        prob_rows = keep.tile([P, P], F32)
+        nc.vector.tensor_copy(out=prob_rows[:], in_=prob_ps[:, 0:P])
+        nc.sync.dma_start(
+            out=out_0.rearrange("b k (s h) w -> (b k s) (h w)", s=PIXEL_TILES),
+            in_=prob_rows[0 : IMAGES * CLASSES * PIXEL_TILES, :],
+        )

@@ -25,9 +25,9 @@ ROUNDS = CLASSES * IMAGES // PAIR
 C_TILES = CHANNELS // P
 PIXEL_TILES = PIXELS // P
 PLANES_PER_TILE = 4
-RUN = 4
 LOADS_AHEAD = 6
-VECTOR_BANKS = 3
+ADDED_IN_PSUM = 2
+HEAD_ROUNDS = 2
 REDUCTION = -0.1
 CLAMP = 500.0
 
@@ -42,14 +42,15 @@ def tile_cssrclassifier_pa_e_kernel(tc, d, W_dec_words, W_dec_scales, x, out_0, 
         raw_pool = ctx.enter_context(tc.tile_pool(name="raw", bufs=LOADS_AHEAD))
         quant_pool = ctx.enter_context(tc.tile_pool(name="quant", bufs=3))
         recon_pool = ctx.enter_context(tc.tile_pool(name="recon", bufs=6))
+        diff_pool = ctx.enter_context(tc.tile_pool(name="diff", bufs=3))
         unread_pool = ctx.enter_context(tc.tile_pool(name="unread", bufs=4))
         recon_psum = ctx.enter_context(tc.psum_pool(name="recon_psum", bufs=4))
         diff_psum = ctx.enter_context(tc.psum_pool(name="diff_psum", bufs=4))
 
         w_codes = keep.tile([P, CLASSES, CHANNELS], U32, align_bytes=64)
         w_planes = keep.tile([P, CLASSES // PLANES_PER_TILE, CHANNELS], U8, align_bytes=64)
-        x_raw = keep.tile([P, IMAGES * C_TILES, PIXELS], BF16)
-        neg_x = keep.tile([P, IMAGES * C_TILES, PIXELS], F32)
+        x_raw = keep.tile([P, IMAGES, C_TILES, PIXELS], BF16)
+        neg_x = keep.tile([P, IMAGES, ADDED_IN_PSUM, PIXELS], F32)
         ident = keep.tile([P, P], F32)
         ones = keep.tile([P, P], F32)
         prob_cols = keep.tile([P, P], F32)
@@ -68,6 +69,7 @@ def tile_cssrclassifier_pa_e_kernel(tc, d, W_dec_words, W_dec_scales, x, out_0, 
         d_codes = {}
         d_scales = {}
         recon_sb = {}
+        diff_sb = {}
 
         def load(j):
             k, pair = divmod(j, IMAGES // PAIR)
@@ -92,25 +94,27 @@ def tile_cssrclassifier_pa_e_kernel(tc, d, W_dec_words, W_dec_scales, x, out_0, 
             )
 
         def load_x(pair):
-            rows = slice(PAIR * pair * C_TILES, PAIR * (pair + 1) * C_TILES)
+            images = slice(PAIR * pair, PAIR * (pair + 1))
             nc.sync.dma_start(
-                out=x_raw[:, rows, :],
-                in_=x[PAIR * pair : PAIR * (pair + 1)].rearrange("b (ct p) h w -> p (b ct) (h w)", p=P),
+                out=x_raw[:, images].rearrange("p b ct w -> p (b ct) w"),
+                in_=x[images].rearrange("b (ct p) h w -> p (b ct) (h w)", p=P),
             )
 
         def negate_x(pair):
-            for b in range(PAIR * pair, PAIR * (pair + 1)):
-                rows = slice(b * C_TILES, (b + 1) * C_TILES)
-                nc.gpsimd.tensor_scalar(
-                    out=neg_x[:, rows, :], in0=x_raw[:, rows, :], scalar1=-1.0, scalar2=0.0, op0=ALU.mult, op1=ALU.add
-                )
+            images = slice(PAIR * pair, PAIR * (pair + 1))
+            nc.scalar.mul(out=neg_x[:, images], in_=x_raw[:, images, 0:ADDED_IN_PSUM, :], mul=-1.0)
 
-        def regroup(j):
-            grouped = quant_pool.tile([P, PAIR * PIXELS, PACK], BF16, align_bytes=64)
-            to_view = grouped[:].rearrange("p (b c i) t -> p b c t i", b=PAIR, i=RUN)
-            from_view = d_raw[j][:].rearrange("p b (t c i) -> p b c t i", t=PACK, i=RUN)
+        def regroup(j, engine):
+            grouped = quant_pool.tile([P, PAIR, PIXELS, PACK], BF16, align_bytes=64)
             for b2 in range(PAIR):
-                nc.vector.tensor_copy(out=to_view[:, b2], in_=from_view[:, b2])
+                engine.tensor_scalar(
+                    out=grouped[:, b2],
+                    in0=d_raw[j][:, b2, :].rearrange("p (t w) -> p w t", t=PACK),
+                    scalar1=1.0,
+                    scalar2=0.0,
+                    op0=ALU.mult,
+                    op1=ALU.add,
+                )
             d_grouped[j] = grouped
 
         def quantise(j):
@@ -119,16 +123,18 @@ def tile_cssrclassifier_pa_e_kernel(tc, d, W_dec_words, W_dec_scales, x, out_0, 
             nc.vector.quantize_mx(
                 out=codes[:].bitcast(FP8X4),
                 scales=scales[:],
-                in_=d_grouped[j][:].rearrange("p w t -> p (w t)"),
+                in_=d_grouped[j][:].rearrange("p b w t -> p (b w t)"),
             )
             d_codes[j] = codes
             d_scales[j] = scales
 
         def multiply(j):
             k, pair = divmod(j, IMAGES // PAIR)
+            images = slice(PAIR * pair, PAIR * (pair + 1))
             offset = 4 * (k % PLANES_PER_TILE)
             group = k // PLANES_PER_TILE
             recon = recon_pool.tile([P, PAIR, C_TILES, PIXELS], F32)
+            diff = diff_pool.tile([P, PAIR, C_TILES - ADDED_IN_PSUM, PIXELS], F32)
             for ct in range(C_TILES):
                 cols = slice(ct * P, (ct + 1) * P)
                 recon_ps = recon_psum.tile([P, PAIR * PIXELS], F32)
@@ -142,16 +148,22 @@ def tile_cssrclassifier_pa_e_kernel(tc, d, W_dec_words, W_dec_scales, x, out_0, 
                     stop=True,
                 )
                 by_image = recon_ps[:].rearrange("p (b w) -> p b w", b=PAIR)
-                if ct < VECTOR_BANKS:
-                    nc.vector.tensor_copy(out=recon[:, :, ct, :], in_=by_image)
-                else:
+                if ct >= ADDED_IN_PSUM:
+                    nc.vector.tensor_tensor(
+                        out=diff[:, :, ct - ADDED_IN_PSUM, :], in0=by_image, in1=x_raw[:, images, ct, :],
+                        op=ALU.subtract,
+                    )
+                if ct == 0:
                     nc.scalar.copy(out=recon[:, :, ct, :], in_=by_image)
+                else:
+                    nc.vector.tensor_copy(out=recon[:, :, ct, :], in_=by_image)
             for b2 in range(PAIR):
                 nc.sync.dma_start(
                     out=out_2[PAIR * pair + b2, k].rearrange("(ct p) h w -> p ct (h w)", p=P),
                     in_=recon[:, b2, :, :],
                 )
             recon_sb[j] = recon
+            diff_sb[j] = diff
 
         def l1_error(j):
             k, pair = divmod(j, IMAGES // PAIR)
@@ -162,40 +174,45 @@ def tile_cssrclassifier_pa_e_kernel(tc, d, W_dec_words, W_dec_scales, x, out_0, 
                     diff_ps = diff_psum.tile([P, CHANNELS], F32)
                     for ct in range(C_TILES):
                         block = diff_ps[:, ct * P : (ct + 1) * P]
-                        nc.tensor.matmul(
-                            out=block, lhsT=neg_x[:, b * C_TILES + ct, pixels], rhs=ident[:],
-                            is_transpose=True, start=True, stop=False,
-                        )
-                        nc.tensor.matmul(
-                            out=block, lhsT=recon_sb[j][:, b2, ct, pixels], rhs=ident[:],
-                            is_transpose=True, start=False, stop=True,
-                        )
+                        if ct < ADDED_IN_PSUM:
+                            nc.tensor.matmul(
+                                out=block, lhsT=neg_x[:, b, ct, pixels], rhs=ident[:],
+                                is_transpose=True, start=True, stop=False,
+                            )
+                            nc.tensor.matmul(
+                                out=block, lhsT=recon_sb[j][:, b2, ct, pixels], rhs=ident[:],
+                                is_transpose=True, start=False, stop=True,
+                            )
+                        else:
+                            nc.tensor.transpose(
+                                out=block, in_=diff_sb[j][:, b2, ct - ADDED_IN_PSUM, pixels], identity=ident[:]
+                            )
                     unread = unread_pool.tile([P, CHANNELS], BF16)
                     nc.scalar.activation(
                         out=unread[:], in_=diff_ps[:], func=ACT.Abs, accum_out=abs_sums[:, b, half, k : k + 1]
                     )
 
         load(0)
-        load(1)
         load_x(0)
+        load(1)
         load(2)
         load_x(1)
         for j in range(3, LOADS_AHEAD):
             load(j)
-        regroup(0)
+        regroup(0, nc.vector)
         quantise(0)
-        regroup(1)
-        negate_x(0)
-        negate_x(1)
+        regroup(1, nc.vector)
         for j in range(ROUNDS + 1):
             if j + LOADS_AHEAD < ROUNDS:
                 load(j + LOADS_AHEAD)
-            if j + 2 < ROUNDS:
-                regroup(j + 2)
             if j + 1 < ROUNDS:
                 quantise(j + 1)
             if j < ROUNDS:
                 multiply(j)
+            if j < IMAGES // PAIR:
+                negate_x(j)
+            if j + HEAD_ROUNDS < ROUNDS:
+                regroup(j + HEAD_ROUNDS, nc.gpsimd)
             if j >= 1:
                 l1_error(j - 1)
 

@@ -47,6 +47,8 @@ def tile_cssrclassifier_pa_e_kernel(tc, d, W_dec_words, W_dec_scales, x, out_0, 
         recon_psum = ctx.enter_context(tc.psum_pool(name="recon_psum", bufs=4))
         diff_psum = ctx.enter_context(tc.psum_pool(name="diff_psum", bufs=4))
 
+        w_codes_raw = keep.tile([P, CLASSES, CHANNELS], U32)
+        w_planes_raw = keep.tile([P, CLASSES // PLANES_PER_TILE, CHANNELS], U8)
         w_codes = keep.tile([P, CLASSES, CHANNELS], U32, align_bytes=64)
         w_planes = keep.tile([P, CLASSES // PLANES_PER_TILE, CHANNELS], U8, align_bytes=64)
         x_raw = keep.tile([P, IMAGES, C_TILES, PIXELS], BF16)
@@ -57,7 +59,7 @@ def tile_cssrclassifier_pa_e_kernel(tc, d, W_dec_words, W_dec_scales, x, out_0, 
         abs_sums = keep.tile([P, IMAGES, PIXEL_TILES, CLASSES], F32)
         warm = keep.tile([P, 2], F32)
 
-        nc.vector.memset(w_planes[:].bitcast(I32), 0)
+        nc.vector.memset(w_planes_raw[:].bitcast(I32), 0)
         nc.vector.memset(warm[:], 0.0)
         nc.scalar.activation(out=warm[:, 1:2], in_=warm[:, 0:1], func=ACT.Exp)
         make_identity(nc, ident[:])
@@ -85,19 +87,31 @@ def tile_cssrclassifier_pa_e_kernel(tc, d, W_dec_words, W_dec_scales, x, out_0, 
                 group = k // PLANES_PER_TILE
                 for quadrant in range(4):
                     nc.sync.dma_start(
-                        out=w_planes[32 * quadrant : 32 * quadrant + 16, group, :].bitcast(I32),
+                        out=w_planes_raw[32 * quadrant : 32 * quadrant + 16, group, :].bitcast(I32),
                         in_=W_dec_scales[k : k + PLANES_PER_TILE, 4 * quadrant : 4 * quadrant + 4, :].bitcast(I32),
                     )
             nc.sync.dma_start(
-                out=w_codes[:, k, :].bitcast(I32),
+                out=w_codes_raw[:, k, :].bitcast(I32),
                 in_=W_dec_words[k].rearrange("p n t -> p (n t)").bitcast(I32),
             )
 
         def load_x(pair):
             images = slice(PAIR * pair, PAIR * (pair + 1))
             nc.sync.dma_start(
-                out=x_raw[:, images].rearrange("p b ct w -> p (b ct) w"),
-                in_=x[images].rearrange("b (ct p) h w -> p (b ct) (h w)", p=P),
+                out=x_raw[:, images].rearrange("p b ct w -> p b (ct w)"),
+                in_=x[images].rearrange("b (p ct) h w -> p b (ct h w)", p=P),
+            )
+
+        def permute_codes(k, engine):
+            engine.tensor_copy(
+                out=w_codes[:, k, :].bitcast(I32).rearrange("p (ct m) -> p ct m", ct=C_TILES),
+                in_=w_codes_raw[:, k, :].bitcast(I32).rearrange("p (m ct) -> p ct m", ct=C_TILES),
+            )
+
+        def permute_planes(group, engine):
+            engine.tensor_copy(
+                out=w_planes[:, group, :].rearrange("p (ct m) -> p m ct", ct=C_TILES),
+                in_=w_planes_raw[:, group, :].rearrange("p (m ct) -> p m ct", ct=C_TILES),
             )
 
         def negate_x(pair):
@@ -159,8 +173,8 @@ def tile_cssrclassifier_pa_e_kernel(tc, d, W_dec_words, W_dec_scales, x, out_0, 
                     nc.vector.tensor_copy(out=recon[:, :, ct, :], in_=by_image)
             for b2 in range(PAIR):
                 nc.sync.dma_start(
-                    out=out_2[PAIR * pair + b2, k].rearrange("(ct p) h w -> p ct (h w)", p=P),
-                    in_=recon[:, b2, :, :],
+                    out=out_2[PAIR * pair + b2, k].rearrange("(p ct) h w -> p (ct h w)", p=P),
+                    in_=recon[:, b2, :, :].rearrange("p ct w -> p (ct w)"),
                 )
             recon_sb[j] = recon
             diff_sb[j] = diff
@@ -200,6 +214,8 @@ def tile_cssrclassifier_pa_e_kernel(tc, d, W_dec_words, W_dec_scales, x, out_0, 
         for j in range(3, LOADS_AHEAD):
             load(j)
         regroup(0, nc.vector)
+        permute_planes(0, nc.vector)
+        permute_codes(0, nc.vector)
         quantise(0)
         regroup(1, nc.vector)
         for j in range(ROUNDS + 1):
@@ -213,6 +229,10 @@ def tile_cssrclassifier_pa_e_kernel(tc, d, W_dec_words, W_dec_scales, x, out_0, 
                 negate_x(j)
             if j + HEAD_ROUNDS < ROUNDS:
                 regroup(j + HEAD_ROUNDS, nc.gpsimd)
+            if j % (IMAGES // PAIR) == 0 and j // (IMAGES // PAIR) + 1 < CLASSES:
+                permute_codes(j // (IMAGES // PAIR) + 1, nc.gpsimd)
+            if j == PLANES_PER_TILE:
+                permute_planes(1, nc.gpsimd)
             if j >= 1:
                 l1_error(j - 1)
 

@@ -26,7 +26,6 @@ C_TILES = CHANNELS // P
 PIXEL_TILES = PIXELS // P
 PLANES_PER_TILE = 4
 LOADS_AHEAD = 6
-ADDED_IN_PSUM = 2
 HEAD_ROUNDS = 2
 REDUCTION = -0.1
 CLAMP = 500.0
@@ -45,15 +44,16 @@ def tile_cssrclassifier_pa_e_kernel(tc, d, W_dec_words, W_dec_scales, x, out_0, 
         diff_pool = ctx.enter_context(tc.tile_pool(name="diff", bufs=3))
         unread_pool = ctx.enter_context(tc.tile_pool(name="unread", bufs=4))
         recon_psum = ctx.enter_context(tc.psum_pool(name="recon_psum", bufs=4))
-        diff_psum = ctx.enter_context(tc.psum_pool(name="diff_psum", bufs=4))
+        turned_psum = ctx.enter_context(tc.psum_pool(name="turned_psum", bufs=4))
 
         w_codes_raw = keep.tile([P, CLASSES, CHANNELS], U32)
         w_planes_raw = keep.tile([P, CLASSES // PLANES_PER_TILE, CHANNELS], U8)
         w_codes = keep.tile([P, CLASSES, CHANNELS], U32, align_bytes=64)
         w_planes = keep.tile([P, CLASSES // PLANES_PER_TILE, CHANNELS], U8, align_bytes=64)
         x_raw = keep.tile([P, IMAGES, C_TILES, PIXELS], BF16)
-        neg_x = keep.tile([P, IMAGES, ADDED_IN_PSUM, PIXELS], F32)
+        x_turned = keep.tile([P, IMAGES, PIXEL_TILES, CHANNELS], BF16)
         ident = keep.tile([P, P], F32)
+        ident_bf = keep.tile([P, P], BF16)
         ones = keep.tile([P, P], F32)
         prob_cols = keep.tile([P, P], F32)
         abs_sums = keep.tile([P, IMAGES, PIXEL_TILES, CLASSES], F32)
@@ -62,6 +62,7 @@ def tile_cssrclassifier_pa_e_kernel(tc, d, W_dec_words, W_dec_scales, x, out_0, 
         nc.vector.memset(w_planes_raw[:].bitcast(I32), 0)
         nc.vector.memset(warm[:], 0.0)
         nc.scalar.activation(out=warm[:, 1:2], in_=warm[:, 0:1], func=ACT.Exp)
+        make_identity(nc, ident_bf[:])
         make_identity(nc, ident[:])
         nc.gpsimd.memset(ones[:], 1.0)
         nc.gpsimd.memset(prob_cols[:], 0.0)
@@ -70,8 +71,6 @@ def tile_cssrclassifier_pa_e_kernel(tc, d, W_dec_words, W_dec_scales, x, out_0, 
         d_grouped = {}
         d_codes = {}
         d_scales = {}
-        recon_sb = {}
-        diff_sb = {}
 
         def load(j):
             k, pair = divmod(j, IMAGES // PAIR)
@@ -114,9 +113,17 @@ def tile_cssrclassifier_pa_e_kernel(tc, d, W_dec_words, W_dec_scales, x, out_0, 
                 in_=w_planes_raw[:, group, :].rearrange("p (m ct) -> p m ct", ct=C_TILES),
             )
 
-        def negate_x(pair):
-            images = slice(PAIR * pair, PAIR * (pair + 1))
-            nc.scalar.mul(out=neg_x[:, images], in_=x_raw[:, images, 0:ADDED_IN_PSUM, :], mul=-1.0)
+        def turn_x(pair):
+            for b in range(PAIR * pair, PAIR * (pair + 1)):
+                for half in range(PIXEL_TILES):
+                    pixels = slice(half * P, (half + 1) * P)
+                    turned_ps = turned_psum.tile([P, CHANNELS], F32)
+                    as_bf16 = turned_ps[:].bitcast(BF16)
+                    for ct in range(C_TILES):
+                        nc.tensor.transpose(
+                            out=as_bf16[:, ct * P : (ct + 1) * P], in_=x_raw[:, b, ct, pixels], identity=ident_bf[:]
+                        )
+                    nc.scalar.copy(out=x_turned[:, b, half, :], in_=as_bf16[:, 0:CHANNELS])
 
         def regroup(j, engine):
             grouped = quant_pool.tile([P, PAIR, PIXELS, PACK], BF16, align_bytes=64)
@@ -144,13 +151,14 @@ def tile_cssrclassifier_pa_e_kernel(tc, d, W_dec_words, W_dec_scales, x, out_0, 
 
         def multiply(j):
             k, pair = divmod(j, IMAGES // PAIR)
-            images = slice(PAIR * pair, PAIR * (pair + 1))
             offset = 4 * (k % PLANES_PER_TILE)
             group = k // PLANES_PER_TILE
             recon = recon_pool.tile([P, PAIR, C_TILES, PIXELS], F32)
-            diff = diff_pool.tile([P, PAIR, C_TILES - ADDED_IN_PSUM, PIXELS], F32)
-            for ct in range(C_TILES):
-                cols = slice(ct * P, (ct + 1) * P)
+            diff = diff_pool.tile([P, PAIR * PIXEL_TILES, CHANNELS], F32)
+            recon_banks = []
+            turned_banks = []
+            for i in range(C_TILES):
+                cols = slice(i * P, (i + 1) * P)
                 recon_ps = recon_psum.tile([P, PAIR * PIXELS], F32)
                 nc.tensor.matmul_mx(
                     out=recon_ps[:],
@@ -161,50 +169,45 @@ def tile_cssrclassifier_pa_e_kernel(tc, d, W_dec_words, W_dec_scales, x, out_0, 
                     start=True,
                     stop=True,
                 )
-                by_image = recon_ps[:].rearrange("p (b w) -> p b w", b=PAIR)
-                if ct >= ADDED_IN_PSUM:
-                    nc.vector.tensor_tensor(
-                        out=diff[:, :, ct - ADDED_IN_PSUM, :], in0=by_image, in1=x_raw[:, images, ct, :],
-                        op=ALU.subtract,
-                    )
-                if ct == 0:
-                    nc.scalar.copy(out=recon[:, :, ct, :], in_=by_image)
-                else:
-                    nc.vector.tensor_copy(out=recon[:, :, ct, :], in_=by_image)
+                recon_banks.append(recon_ps)
+                turned_ps = turned_psum.tile([P, CHANNELS], F32)
+                nc.tensor.matmul_mx(
+                    out=turned_ps[:],
+                    lhsT=d_codes[j][:, cols].bitcast(FP8X4),
+                    lhsT_scale=d_scales[j][:, cols],
+                    rhs=w_codes[:, k, :].bitcast(FP8X4),
+                    rhs_scale=w_planes[offset:P, group, :],
+                    start=True,
+                    stop=True,
+                )
+                turned_banks.append(turned_ps)
+            scalar_copies = 2 + j % 2
+            for ct in range(scalar_copies):
+                nc.scalar.copy(
+                    out=recon[:, :, ct, :], in_=recon_banks[ct][:].rearrange("p (b w) -> p b w", b=PAIR)
+                )
+            for i in range(PAIR * PIXEL_TILES):
+                b2, half = divmod(i, PIXEL_TILES)
+                nc.vector.tensor_tensor(
+                    out=diff[:, i, :], in0=turned_banks[i][:], in1=x_turned[:, PAIR * pair + b2, half, :],
+                    op=ALU.subtract,
+                )
+            for ct in range(scalar_copies, C_TILES):
+                nc.vector.tensor_copy(
+                    out=recon[:, :, ct, :], in_=recon_banks[ct][:].rearrange("p (b w) -> p b w", b=PAIR)
+                )
+            for i in range(PAIR * PIXEL_TILES):
+                b2, half = divmod(i, PIXEL_TILES)
+                unread = unread_pool.tile([P, CHANNELS], BF16)
+                nc.scalar.activation(
+                    out=unread[:], in_=diff[:, i, :], func=ACT.Abs,
+                    accum_out=abs_sums[:, PAIR * pair + b2, half, k : k + 1],
+                )
             for b2 in range(PAIR):
                 nc.sync.dma_start(
                     out=out_2[PAIR * pair + b2, k].rearrange("(p ct) h w -> p (ct h w)", p=P),
                     in_=recon[:, b2, :, :].rearrange("p ct w -> p (ct w)"),
                 )
-            recon_sb[j] = recon
-            diff_sb[j] = diff
-
-        def l1_error(j):
-            k, pair = divmod(j, IMAGES // PAIR)
-            for b2 in range(PAIR):
-                b = PAIR * pair + b2
-                for half in range(PIXEL_TILES):
-                    pixels = slice(half * P, (half + 1) * P)
-                    diff_ps = diff_psum.tile([P, CHANNELS], F32)
-                    for ct in range(C_TILES):
-                        block = diff_ps[:, ct * P : (ct + 1) * P]
-                        if ct < ADDED_IN_PSUM:
-                            nc.tensor.matmul(
-                                out=block, lhsT=neg_x[:, b, ct, pixels], rhs=ident[:],
-                                is_transpose=True, start=True, stop=False,
-                            )
-                            nc.tensor.matmul(
-                                out=block, lhsT=recon_sb[j][:, b2, ct, pixels], rhs=ident[:],
-                                is_transpose=True, start=False, stop=True,
-                            )
-                        else:
-                            nc.tensor.transpose(
-                                out=block, in_=diff_sb[j][:, b2, ct - ADDED_IN_PSUM, pixels], identity=ident[:]
-                            )
-                    unread = unread_pool.tile([P, CHANNELS], BF16)
-                    nc.scalar.activation(
-                        out=unread[:], in_=diff_ps[:], func=ACT.Abs, accum_out=abs_sums[:, b, half, k : k + 1]
-                    )
 
         load(0)
         load_x(0)
@@ -218,23 +221,21 @@ def tile_cssrclassifier_pa_e_kernel(tc, d, W_dec_words, W_dec_scales, x, out_0, 
         permute_codes(0, nc.vector)
         quantise(0)
         regroup(1, nc.vector)
-        for j in range(ROUNDS + 1):
+        turn_x(0)
+        for j in range(ROUNDS):
             if j + LOADS_AHEAD < ROUNDS:
                 load(j + LOADS_AHEAD)
             if j + 1 < ROUNDS:
                 quantise(j + 1)
-            if j < ROUNDS:
-                multiply(j)
-            if j < IMAGES // PAIR:
-                negate_x(j)
+            multiply(j)
+            if j == 0:
+                turn_x(1)
             if j + HEAD_ROUNDS < ROUNDS:
                 regroup(j + HEAD_ROUNDS, nc.gpsimd)
             if j % (IMAGES // PAIR) == 0 and j // (IMAGES // PAIR) + 1 < CLASSES:
                 permute_codes(j // (IMAGES // PAIR) + 1, nc.gpsimd)
             if j == PLANES_PER_TILE:
                 permute_planes(1, nc.gpsimd)
-            if j >= 1:
-                l1_error(j - 1)
 
         logits = keep.tile([P, IMAGES, PIXEL_TILES, CLASSES], F32)
         nc.vector.tensor_scalar(
@@ -244,7 +245,7 @@ def tile_cssrclassifier_pa_e_kernel(tc, d, W_dec_words, W_dec_scales, x, out_0, 
 
         halves = keep.tile([P, IMAGES, CLASSES], F32)
         nc.vector.tensor_tensor(out=halves[:], in0=logits[:, :, 0, :], in1=logits[:, :, 1, :], op=ALU.add)
-        mean_ps = diff_psum.tile([P, CHANNELS], F32, tag="diff_ps")
+        mean_ps = turned_psum.tile([P, CHANNELS], F32, tag="turned_ps")
         nc.tensor.matmul(
             out=mean_ps[:, 0 : IMAGES * CLASSES], lhsT=ones[:], rhs=halves[:].rearrange("p b k -> p (b k)"),
             start=True, stop=True,
@@ -279,7 +280,7 @@ def tile_cssrclassifier_pa_e_kernel(tc, d, W_dec_words, W_dec_scales, x, out_0, 
             in1=inverse[:].unsqueeze(3).to_broadcast(group_shape),
             op=ALU.mult,
         )
-        prob_ps = diff_psum.tile([P, CHANNELS], F32, tag="diff_ps")
+        prob_ps = turned_psum.tile([P, CHANNELS], F32, tag="turned_ps")
         nc.tensor.transpose(out=prob_ps[:, 0:P], in_=prob_cols[:], identity=ident[:])
         prob_rows = keep.tile([P, P], F32)
         nc.vector.tensor_copy(out=prob_rows[:], in_=prob_ps[:, 0:P])

@@ -39,6 +39,7 @@ def tile_cssrclassifier_pa_e_kernel(tc, d, W_dec_words, W_dec_scales, x, out_0, 
         ctx.enter_context(tc.manual_schedule())
         keep = ctx.enter_context(tc.tile_pool(name="keep", bufs=1))
         raw_pool = ctx.enter_context(tc.tile_pool(name="raw", bufs=LOADS_AHEAD))
+        grouped_pool = ctx.enter_context(tc.tile_pool(name="grouped", bufs=1))
         quant_pool = ctx.enter_context(tc.tile_pool(name="quant", bufs=3))
         recon_pool = ctx.enter_context(tc.tile_pool(name="recon", bufs=6))
         diff_pool = ctx.enter_context(tc.tile_pool(name="diff", bufs=3))
@@ -126,7 +127,7 @@ def tile_cssrclassifier_pa_e_kernel(tc, d, W_dec_words, W_dec_scales, x, out_0, 
                     nc.scalar.copy(out=x_turned[:, b, half, :], in_=as_bf16[:, 0:CHANNELS])
 
         def regroup(j, engine):
-            grouped = quant_pool.tile([P, PAIR, PIXELS, PACK], BF16, align_bytes=64)
+            grouped = grouped_pool.tile([P, PAIR, PIXELS, PACK], BF16, align_bytes=64)
             for b2 in range(PAIR):
                 engine.tensor_scalar(
                     out=grouped[:, b2],
@@ -227,15 +228,15 @@ def tile_cssrclassifier_pa_e_kernel(tc, d, W_dec_words, W_dec_scales, x, out_0, 
                 load(j + LOADS_AHEAD)
             if j + 1 < ROUNDS:
                 quantise(j + 1)
+            if j % (IMAGES // PAIR) == 0 and j // (IMAGES // PAIR) + 1 < CLASSES:
+                permute_codes(j // (IMAGES // PAIR) + 1, nc.vector)
+            if j == PLANES_PER_TILE:
+                permute_planes(1, nc.vector)
             multiply(j)
             if j == 0:
                 turn_x(1)
             if j + HEAD_ROUNDS < ROUNDS:
                 regroup(j + HEAD_ROUNDS, nc.gpsimd)
-            if j % (IMAGES // PAIR) == 0 and j // (IMAGES // PAIR) + 1 < CLASSES:
-                permute_codes(j // (IMAGES // PAIR) + 1, nc.gpsimd)
-            if j == PLANES_PER_TILE:
-                permute_planes(1, nc.gpsimd)
 
         logits = keep.tile([P, IMAGES, PIXEL_TILES, CLASSES], F32)
         nc.vector.tensor_scalar(

@@ -190,7 +190,7 @@ def tile_cssrclassifier_pa_e_kernel(tc, d, W_dec_words, W_dec_scales, x, out_0, 
             for i in range(PAIR * PIXEL_TILES):
                 b2, half = divmod(i, PIXEL_TILES)
                 nc.vector.tensor_tensor(
-                    out=diff[:, i, :], in0=turned_banks[i][:], in1=x_turned[:, PAIR * pair + b2, half, :],
+                    out=diff[:, i, :], in0=x_turned[:, PAIR * pair + b2, half, :], in1=turned_banks[i][:],
                     op=ALU.subtract,
                 )
             for ct in range(scalar_copies, C_TILES):

@@ -26,7 +26,8 @@ C_TILES = CHANNELS // P
 PIXEL_TILES = PIXELS // P
 PLANES_PER_TILE = 4
 LOADS_AHEAD = 6
-HEAD_ROUNDS = 2
+REGROUP_AHEAD = 3
+VECTOR_PIXELS = 176
 REDUCTION = -0.1
 CLAMP = 500.0
 
@@ -39,13 +40,13 @@ def tile_cssrclassifier_pa_e_kernel(tc, d, W_dec_words, W_dec_scales, x, out_0, 
         ctx.enter_context(tc.manual_schedule())
         keep = ctx.enter_context(tc.tile_pool(name="keep", bufs=1))
         raw_pool = ctx.enter_context(tc.tile_pool(name="raw", bufs=LOADS_AHEAD))
-        grouped_pool = ctx.enter_context(tc.tile_pool(name="grouped", bufs=1))
+        grouped_pool = ctx.enter_context(tc.tile_pool(name="grouped", bufs=3))
         quant_pool = ctx.enter_context(tc.tile_pool(name="quant", bufs=3))
         recon_pool = ctx.enter_context(tc.tile_pool(name="recon", bufs=6))
-        diff_pool = ctx.enter_context(tc.tile_pool(name="diff", bufs=3))
-        unread_pool = ctx.enter_context(tc.tile_pool(name="unread", bufs=4))
-        recon_psum = ctx.enter_context(tc.psum_pool(name="recon_psum", bufs=4))
-        turned_psum = ctx.enter_context(tc.psum_pool(name="turned_psum", bufs=4))
+        unread_pool = ctx.enter_context(tc.tile_pool(name="unread", bufs=2))
+        recon_psum = ctx.enter_context(tc.psum_pool(name="recon_psum", bufs=3))
+        turned_psum = ctx.enter_context(tc.psum_pool(name="turned_psum", bufs=3))
+        folded_psum = ctx.enter_context(tc.psum_pool(name="folded_psum", bufs=2))
 
         w_codes_raw = keep.tile([P, CLASSES, CHANNELS], U32)
         w_planes_raw = keep.tile([P, CLASSES // PLANES_PER_TILE, CHANNELS], U8)
@@ -57,7 +58,9 @@ def tile_cssrclassifier_pa_e_kernel(tc, d, W_dec_words, W_dec_scales, x, out_0, 
         ident_bf = keep.tile([P, P], BF16)
         ones = keep.tile([P, P], F32)
         prob_cols = keep.tile([P, P], F32)
-        abs_sums = keep.tile([P, IMAGES, PIXEL_TILES, CLASSES], F32)
+        max_sums = keep.tile([P, IMAGES, PIXEL_TILES, CLASSES], F32)
+        recon_sums = keep.tile([P, IMAGES, PIXEL_TILES, CLASSES], F32)
+        x_sums = keep.tile([P, IMAGES, PIXEL_TILES], F32)
         warm = keep.tile([P, 2], F32)
 
         nc.vector.memset(w_planes_raw[:].bitcast(I32), 0)
@@ -124,20 +127,25 @@ def tile_cssrclassifier_pa_e_kernel(tc, d, W_dec_words, W_dec_scales, x, out_0, 
                         nc.tensor.transpose(
                             out=as_bf16[:, ct * P : (ct + 1) * P], in_=x_raw[:, b, ct, pixels], identity=ident_bf[:]
                         )
-                    nc.scalar.copy(out=x_turned[:, b, half, :], in_=as_bf16[:, 0:CHANNELS])
+                    nc.scalar.activation(
+                        out=x_turned[:, b, half, :], in_=as_bf16[:, 0:CHANNELS], func=ACT.Copy,
+                        accum_out=x_sums[:, b, half : half + 1],
+                    )
 
-        def regroup(j, engine):
-            grouped = grouped_pool.tile([P, PAIR, PIXELS, PACK], BF16, align_bytes=64)
-            for b2 in range(PAIR):
-                engine.tensor_scalar(
-                    out=grouped[:, b2],
-                    in0=d_raw[j][:, b2, :].rearrange("p (t w) -> p w t", t=PACK),
-                    scalar1=1.0,
-                    scalar2=0.0,
-                    op0=ALU.mult,
-                    op1=ALU.add,
-                )
-            d_grouped[j] = grouped
+        def regroup_vector(j, first, last):
+            if j not in d_grouped:
+                grouped = grouped_pool.tile([P, PAIR, PIXELS, PACK], BF16, align_bytes=64)
+                d_grouped[j] = grouped
+            nc.vector.tensor_copy(
+                out=d_grouped[j][:, :, first:last, :],
+                in_=d_raw[j][:].rearrange("p b (t w) -> p b w t", t=PACK)[:, :, first:last, :],
+            )
+
+        def regroup_scalar(j, first, last):
+            nc.scalar.copy(
+                out=d_grouped[j][:, :, first:last, :],
+                in_=d_raw[j][:].rearrange("p b (t w) -> p b w t", t=PACK)[:, :, first:last, :],
+            )
 
         def quantise(j):
             codes = quant_pool.tile([P, PAIR * PIXELS], U32, align_bytes=64)
@@ -155,11 +163,11 @@ def tile_cssrclassifier_pa_e_kernel(tc, d, W_dec_words, W_dec_scales, x, out_0, 
             offset = 4 * (k % PLANES_PER_TILE)
             group = k // PLANES_PER_TILE
             recon = recon_pool.tile([P, PAIR, C_TILES, PIXELS], F32)
-            diff = diff_pool.tile([P, PAIR * PIXEL_TILES, CHANNELS], F32)
-            recon_banks = []
-            turned_banks = []
+            folded_ps = folded_psum.tile([P, PAIR * PIXEL_TILES, P], F32)
             for i in range(C_TILES):
                 cols = slice(i * P, (i + 1) * P)
+                b2, half = divmod(i, PIXEL_TILES)
+                b = PAIR * pair + b2
                 recon_ps = recon_psum.tile([P, PAIR * PIXELS], F32)
                 nc.tensor.matmul_mx(
                     out=recon_ps[:],
@@ -170,7 +178,7 @@ def tile_cssrclassifier_pa_e_kernel(tc, d, W_dec_words, W_dec_scales, x, out_0, 
                     start=True,
                     stop=True,
                 )
-                recon_banks.append(recon_ps)
+                nc.scalar.copy(out=recon[:, :, i, :], in_=recon_ps[:].rearrange("p (b w) -> p b w", b=PAIR))
                 turned_ps = turned_psum.tile([P, CHANNELS], F32)
                 nc.tensor.matmul_mx(
                     out=turned_ps[:],
@@ -181,28 +189,27 @@ def tile_cssrclassifier_pa_e_kernel(tc, d, W_dec_words, W_dec_scales, x, out_0, 
                     start=True,
                     stop=True,
                 )
-                turned_banks.append(turned_ps)
-            scalar_copies = 2 + j % 2
-            for ct in range(scalar_copies):
-                nc.scalar.copy(
-                    out=recon[:, :, ct, :], in_=recon_banks[ct][:].rearrange("p (b w) -> p b w", b=PAIR)
+                unread = unread_pool.tile([P, CHANNELS], F32)
+                nc.vector.scalar_tensor_tensor(
+                    out=unread[:], in0=turned_ps[:], scalar=1.0, in1=x_turned[:, b, half, :],
+                    op0=ALU.mult, op1=ALU.max, accum_out=max_sums[:, b, half, k : k + 1],
                 )
+                for ct in range(C_TILES):
+                    nc.tensor.matmul_mx(
+                        out=folded_ps[:, i, :],
+                        lhsT=d_codes[j][:, cols].bitcast(FP8X4),
+                        lhsT_scale=d_scales[j][:, cols],
+                        rhs=w_codes[:, k, ct * P : (ct + 1) * P].bitcast(FP8X4),
+                        rhs_scale=w_planes[offset:P, group, ct * P : (ct + 1) * P],
+                        start=(ct == 0),
+                        stop=(ct == C_TILES - 1),
+                    )
             for i in range(PAIR * PIXEL_TILES):
                 b2, half = divmod(i, PIXEL_TILES)
-                nc.vector.tensor_tensor(
-                    out=diff[:, i, :], in0=x_turned[:, PAIR * pair + b2, half, :], in1=turned_banks[i][:],
-                    op=ALU.subtract,
-                )
-            for ct in range(scalar_copies, C_TILES):
-                nc.vector.tensor_copy(
-                    out=recon[:, :, ct, :], in_=recon_banks[ct][:].rearrange("p (b w) -> p b w", b=PAIR)
-                )
-            for i in range(PAIR * PIXEL_TILES):
-                b2, half = divmod(i, PIXEL_TILES)
-                unread = unread_pool.tile([P, CHANNELS], BF16)
+                unread_s = unread_pool.tile([P, P], BF16)
                 nc.scalar.activation(
-                    out=unread[:], in_=diff[:, i, :], func=ACT.Abs,
-                    accum_out=abs_sums[:, PAIR * pair + b2, half, k : k + 1],
+                    out=unread_s[:], in_=folded_ps[:, i, :], func=ACT.Copy,
+                    accum_out=recon_sums[:, PAIR * pair + b2, half, k : k + 1],
                 )
             for b2 in range(PAIR):
                 nc.sync.dma_start(
@@ -217,11 +224,13 @@ def tile_cssrclassifier_pa_e_kernel(tc, d, W_dec_words, W_dec_scales, x, out_0, 
         load_x(1)
         for j in range(3, LOADS_AHEAD):
             load(j)
-        regroup(0, nc.vector)
+        regroup_vector(0, 0, VECTOR_PIXELS)
+        regroup_scalar(0, VECTOR_PIXELS, PIXELS)
         permute_planes(0, nc.vector)
         permute_codes(0, nc.vector)
         quantise(0)
-        regroup(1, nc.vector)
+        regroup_vector(1, 0, VECTOR_PIXELS)
+        regroup_scalar(1, VECTOR_PIXELS, PIXELS)
         turn_x(0)
         for j in range(ROUNDS):
             if j + LOADS_AHEAD < ROUNDS:
@@ -235,8 +244,19 @@ def tile_cssrclassifier_pa_e_kernel(tc, d, W_dec_words, W_dec_scales, x, out_0, 
             multiply(j)
             if j == 0:
                 turn_x(1)
-            if j + HEAD_ROUNDS < ROUNDS:
-                regroup(j + HEAD_ROUNDS, nc.gpsimd)
+            for r in range(REGROUP_AHEAD - 1 if j == 0 else j + REGROUP_AHEAD, min(j + REGROUP_AHEAD + 1, ROUNDS)):
+                regroup_vector(r, 0, VECTOR_PIXELS)
+                regroup_scalar(r, VECTOR_PIXELS, PIXELS)
+
+        abs_sums = keep.tile([P, IMAGES, PIXEL_TILES, CLASSES], F32)
+        nc.vector.scalar_tensor_tensor(
+            out=abs_sums[:].rearrange("p b s k -> p (b s k)"), in0=max_sums[:].rearrange("p b s k -> p (b s k)"),
+            scalar=2.0, in1=recon_sums[:].rearrange("p b s k -> p (b s k)"), op0=ALU.mult, op1=ALU.subtract,
+        )
+        nc.vector.tensor_tensor(
+            out=abs_sums[:], in0=abs_sums[:],
+            in1=x_sums[:].unsqueeze(3).to_broadcast([P, IMAGES, PIXEL_TILES, CLASSES]), op=ALU.subtract,
+        )
 
         logits = keep.tile([P, IMAGES, PIXEL_TILES, CLASSES], F32)
         nc.vector.tensor_scalar(

@@ -27,7 +27,7 @@ PIXEL_TILES = PIXELS // P
 PLANES_PER_TILE = 4
 LOADS_AHEAD = 6
 REGROUP_AHEAD = 3
-VECTOR_PIXELS = 176
+FIRST_PIXELS = 192
 REDUCTION = -0.1
 CLAMP = 500.0
 
@@ -40,7 +40,7 @@ def tile_cssrclassifier_pa_e_kernel(tc, d, W_dec_words, W_dec_scales, x, out_0, 
         ctx.enter_context(tc.manual_schedule())
         keep = ctx.enter_context(tc.tile_pool(name="keep", bufs=1))
         raw_pool = ctx.enter_context(tc.tile_pool(name="raw", bufs=LOADS_AHEAD))
-        grouped_pool = ctx.enter_context(tc.tile_pool(name="grouped", bufs=3))
+        grouped_pool = ctx.enter_context(tc.tile_pool(name="grouped", bufs=2))
         quant_pool = ctx.enter_context(tc.tile_pool(name="quant", bufs=3))
         recon_pool = ctx.enter_context(tc.tile_pool(name="recon", bufs=6))
         unread_pool = ctx.enter_context(tc.tile_pool(name="unread", bufs=2))
@@ -132,13 +132,16 @@ def tile_cssrclassifier_pa_e_kernel(tc, d, W_dec_words, W_dec_scales, x, out_0, 
                         accum_out=x_sums[:, b, half : half + 1],
                     )
 
-        def regroup_vector(j, first, last):
-            if j not in d_grouped:
-                grouped = grouped_pool.tile([P, PAIR, PIXELS, PACK], BF16, align_bytes=64)
-                d_grouped[j] = grouped
-            nc.vector.tensor_copy(
-                out=d_grouped[j][:, :, first:last, :],
-                in_=d_raw[j][:].rearrange("p b (t w) -> p b w t", t=PACK)[:, :, first:last, :],
+        def regroup_first(j, engine, last):
+            grouped = grouped_pool.tile([P, PAIR, PIXELS, PACK], BF16, align_bytes=64)
+            d_grouped[j] = grouped
+            engine.tensor_scalar(
+                out=grouped[:, :, 0:last, :],
+                in0=d_raw[j][:].rearrange("p b (t w) -> p b w t", t=PACK)[:, :, 0:last, :],
+                scalar1=1.0,
+                scalar2=0.0,
+                op0=ALU.mult,
+                op1=ALU.add,
             )
 
         def regroup_scalar(j, first, last):
@@ -224,29 +227,29 @@ def tile_cssrclassifier_pa_e_kernel(tc, d, W_dec_words, W_dec_scales, x, out_0, 
         load_x(1)
         for j in range(3, LOADS_AHEAD):
             load(j)
-        regroup_vector(0, 0, VECTOR_PIXELS)
-        regroup_scalar(0, VECTOR_PIXELS, PIXELS)
+        regroup_first(0, nc.vector, FIRST_PIXELS)
+        regroup_scalar(0, FIRST_PIXELS, PIXELS)
         permute_planes(0, nc.vector)
         permute_codes(0, nc.vector)
         quantise(0)
-        regroup_vector(1, 0, VECTOR_PIXELS)
-        regroup_scalar(1, VECTOR_PIXELS, PIXELS)
+        regroup_first(1, nc.vector, FIRST_PIXELS)
+        regroup_scalar(1, FIRST_PIXELS, PIXELS)
         turn_x(0)
         for j in range(ROUNDS):
             if j + LOADS_AHEAD < ROUNDS:
                 load(j + LOADS_AHEAD)
             if j + 1 < ROUNDS:
                 quantise(j + 1)
-            if j % (IMAGES // PAIR) == 0 and j // (IMAGES // PAIR) + 1 < CLASSES:
-                permute_codes(j // (IMAGES // PAIR) + 1, nc.vector)
-            if j == PLANES_PER_TILE:
-                permute_planes(1, nc.vector)
             multiply(j)
             if j == 0:
                 turn_x(1)
             for r in range(REGROUP_AHEAD - 1 if j == 0 else j + REGROUP_AHEAD, min(j + REGROUP_AHEAD + 1, ROUNDS)):
-                regroup_vector(r, 0, VECTOR_PIXELS)
-                regroup_scalar(r, VECTOR_PIXELS, PIXELS)
+                regroup_first(r, nc.gpsimd, FIRST_PIXELS)
+                regroup_scalar(r, FIRST_PIXELS, PIXELS)
+            if j % (IMAGES // PAIR) == 0 and j // (IMAGES // PAIR) + 1 < CLASSES:
+                permute_codes(j // (IMAGES // PAIR) + 1, nc.gpsimd)
+            if j == PLANES_PER_TILE:
+                permute_planes(1, nc.gpsimd)
 
         abs_sums = keep.tile([P, IMAGES, PIXEL_TILES, CLASSES], F32)
         nc.vector.scalar_tensor_tensor(

@@ -27,7 +27,7 @@ PIXEL_TILES = PIXELS // P
 PLANES_PER_TILE = 4
 LOADS_AHEAD = 6
 REGROUP_AHEAD = 3
-FIRST_PIXELS = 192
+FIRST_PIXELS = 176
 REDUCTION = -0.1
 CLAMP = 500.0
 
@@ -43,6 +43,7 @@ def tile_cssrclassifier_pa_e_kernel(tc, d, W_dec_words, W_dec_scales, x, out_0, 
         grouped_pool = ctx.enter_context(tc.tile_pool(name="grouped", bufs=2))
         quant_pool = ctx.enter_context(tc.tile_pool(name="quant", bufs=3))
         recon_pool = ctx.enter_context(tc.tile_pool(name="recon", bufs=6))
+        diff_pool = ctx.enter_context(tc.tile_pool(name="diff", bufs=3))
         unread_pool = ctx.enter_context(tc.tile_pool(name="unread", bufs=2))
         recon_psum = ctx.enter_context(tc.psum_pool(name="recon_psum", bufs=3))
         turned_psum = ctx.enter_context(tc.psum_pool(name="turned_psum", bufs=3))
@@ -70,6 +71,8 @@ def tile_cssrclassifier_pa_e_kernel(tc, d, W_dec_words, W_dec_scales, x, out_0, 
         make_identity(nc, ident[:])
         nc.gpsimd.memset(ones[:], 1.0)
         nc.gpsimd.memset(prob_cols[:], 0.0)
+        nc.gpsimd.memset(recon_sums[:], 0.0)
+        nc.gpsimd.memset(x_sums[:], 0.0)
 
         d_raw = {}
         d_grouped = {}
@@ -117,6 +120,9 @@ def tile_cssrclassifier_pa_e_kernel(tc, d, W_dec_words, W_dec_scales, x, out_0, 
                 in_=w_planes_raw[:, group, :].rearrange("p (m ct) -> p m ct", ct=C_TILES),
             )
 
+        def direct(pair, i):
+            return i <= pair
+
         def turn_x(pair):
             for b in range(PAIR * pair, PAIR * (pair + 1)):
                 for half in range(PIXEL_TILES):
@@ -127,10 +133,13 @@ def tile_cssrclassifier_pa_e_kernel(tc, d, W_dec_words, W_dec_scales, x, out_0, 
                         nc.tensor.transpose(
                             out=as_bf16[:, ct * P : (ct + 1) * P], in_=x_raw[:, b, ct, pixels], identity=ident_bf[:]
                         )
-                    nc.scalar.activation(
-                        out=x_turned[:, b, half, :], in_=as_bf16[:, 0:CHANNELS], func=ACT.Copy,
-                        accum_out=x_sums[:, b, half : half + 1],
-                    )
+                    if direct(pair, PIXEL_TILES * (b - PAIR * pair) + half):
+                        nc.scalar.copy(out=x_turned[:, b, half, :], in_=as_bf16[:, 0:CHANNELS])
+                    else:
+                        nc.scalar.activation(
+                            out=x_turned[:, b, half, :], in_=as_bf16[:, 0:CHANNELS], func=ACT.Copy,
+                            accum_out=x_sums[:, b, half : half + 1],
+                        )
 
         def regroup_first(j, engine, last):
             grouped = grouped_pool.tile([P, PAIR, PIXELS, PACK], BF16, align_bytes=64)
@@ -165,12 +174,13 @@ def tile_cssrclassifier_pa_e_kernel(tc, d, W_dec_words, W_dec_scales, x, out_0, 
             k, pair = divmod(j, IMAGES // PAIR)
             offset = 4 * (k % PLANES_PER_TILE)
             group = k // PLANES_PER_TILE
+            last_round = j == ROUNDS - 1
             recon = recon_pool.tile([P, PAIR, C_TILES, PIXELS], F32)
             folded_ps = folded_psum.tile([P, PAIR * PIXEL_TILES, P], F32)
-            for i in range(C_TILES):
+            diffs = {}
+
+            def recon_way(i):
                 cols = slice(i * P, (i + 1) * P)
-                b2, half = divmod(i, PIXEL_TILES)
-                b = PAIR * pair + b2
                 recon_ps = recon_psum.tile([P, PAIR * PIXELS], F32)
                 nc.tensor.matmul_mx(
                     out=recon_ps[:],
@@ -181,7 +191,15 @@ def tile_cssrclassifier_pa_e_kernel(tc, d, W_dec_words, W_dec_scales, x, out_0, 
                     start=True,
                     stop=True,
                 )
-                nc.scalar.copy(out=recon[:, :, i, :], in_=recon_ps[:].rearrange("p (b w) -> p b w", b=PAIR))
+                if pair == 1 and i == C_TILES - 1 and not last_round:
+                    nc.vector.tensor_copy(out=recon[:, :, i, :], in_=recon_ps[:].rearrange("p (b w) -> p b w", b=PAIR))
+                else:
+                    nc.scalar.copy(out=recon[:, :, i, :], in_=recon_ps[:].rearrange("p (b w) -> p b w", b=PAIR))
+
+            def turned_way(i):
+                cols = slice(i * P, (i + 1) * P)
+                b2, half = divmod(i, PIXEL_TILES)
+                b = PAIR * pair + b2
                 turned_ps = turned_psum.tile([P, CHANNELS], F32)
                 nc.tensor.matmul_mx(
                     out=turned_ps[:],
@@ -192,28 +210,56 @@ def tile_cssrclassifier_pa_e_kernel(tc, d, W_dec_words, W_dec_scales, x, out_0, 
                     start=True,
                     stop=True,
                 )
-                unread = unread_pool.tile([P, CHANNELS], F32)
-                nc.vector.scalar_tensor_tensor(
-                    out=unread[:], in0=turned_ps[:], scalar=1.0, in1=x_turned[:, b, half, :],
-                    op0=ALU.mult, op1=ALU.max, accum_out=max_sums[:, b, half, k : k + 1],
-                )
-                for ct in range(C_TILES):
-                    nc.tensor.matmul_mx(
-                        out=folded_ps[:, i, :],
-                        lhsT=d_codes[j][:, cols].bitcast(FP8X4),
-                        lhsT_scale=d_scales[j][:, cols],
-                        rhs=w_codes[:, k, ct * P : (ct + 1) * P].bitcast(FP8X4),
-                        rhs_scale=w_planes[offset:P, group, ct * P : (ct + 1) * P],
-                        start=(ct == 0),
-                        stop=(ct == C_TILES - 1),
+                if direct(pair, i):
+                    diff = diff_pool.tile([P, CHANNELS], F32)
+                    nc.vector.tensor_tensor(
+                        out=diff[:], in0=turned_ps[:], in1=x_turned[:, b, half, :], op=ALU.subtract
                     )
-            for i in range(PAIR * PIXEL_TILES):
-                b2, half = divmod(i, PIXEL_TILES)
-                unread_s = unread_pool.tile([P, P], BF16)
-                nc.scalar.activation(
-                    out=unread_s[:], in_=folded_ps[:, i, :], func=ACT.Copy,
-                    accum_out=recon_sums[:, PAIR * pair + b2, half, k : k + 1],
-                )
+                    diffs[i] = diff
+                else:
+                    unread = unread_pool.tile([P, CHANNELS], F32)
+                    nc.vector.scalar_tensor_tensor(
+                        out=unread[:], in0=turned_ps[:], scalar=1.0, in1=x_turned[:, b, half, :],
+                        op0=ALU.mult, op1=ALU.max, accum_out=max_sums[:, b, half, k : k + 1],
+                    )
+                    for ct in range(C_TILES):
+                        nc.tensor.matmul_mx(
+                            out=folded_ps[:, i, :],
+                            lhsT=d_codes[j][:, cols].bitcast(FP8X4),
+                            lhsT_scale=d_scales[j][:, cols],
+                            rhs=w_codes[:, k, ct * P : (ct + 1) * P].bitcast(FP8X4),
+                            rhs_scale=w_planes[offset:P, group, ct * P : (ct + 1) * P],
+                            start=(ct == 0),
+                            stop=(ct == C_TILES - 1),
+                        )
+
+            def scalar_sums():
+                for i in range(PAIR * PIXEL_TILES):
+                    b2, half = divmod(i, PIXEL_TILES)
+                    if direct(pair, i):
+                        unread_d = unread_pool.tile([P, CHANNELS], BF16)
+                        nc.scalar.activation(
+                            out=unread_d[:], in_=diffs[i][:], func=ACT.Abs, scale=0.5,
+                            accum_out=max_sums[:, PAIR * pair + b2, half, k : k + 1],
+                        )
+                    else:
+                        unread_s = unread_pool.tile([P, P], BF16)
+                        nc.scalar.activation(
+                            out=unread_s[:], in_=folded_ps[:, i, :], func=ACT.Copy,
+                            accum_out=recon_sums[:, PAIR * pair + b2, half, k : k + 1],
+                        )
+
+            if last_round:
+                for i in range(C_TILES):
+                    turned_way(i)
+                scalar_sums()
+                for i in range(C_TILES):
+                    recon_way(i)
+            else:
+                for i in range(C_TILES):
+                    recon_way(i)
+                    turned_way(i)
+                scalar_sums()
             for b2 in range(PAIR):
                 nc.sync.dma_start(
                     out=out_2[PAIR * pair + b2, k].rearrange("(p ct) h w -> p (ct h w)", p=P),
@@ -244,8 +290,7 @@ def tile_cssrclassifier_pa_e_kernel(tc, d, W_dec_words, W_dec_scales, x, out_0, 
             if j == 0:
                 turn_x(1)
             for r in range(REGROUP_AHEAD - 1 if j == 0 else j + REGROUP_AHEAD, min(j + REGROUP_AHEAD + 1, ROUNDS)):
-                regroup_first(r, nc.gpsimd, FIRST_PIXELS)
-                regroup_scalar(r, FIRST_PIXELS, PIXELS)
+                regroup_first(r, nc.gpsimd, PIXELS)
             if j % (IMAGES // PAIR) == 0 and j // (IMAGES // PAIR) + 1 < CLASSES:
                 permute_codes(j // (IMAGES // PAIR) + 1, nc.gpsimd)
             if j == PLANES_PER_TILE:
@@ -265,15 +310,6 @@ def tile_cssrclassifier_pa_e_kernel(tc, d, W_dec_words, W_dec_scales, x, out_0, 
         nc.vector.tensor_scalar(
             out=logits[:], in0=abs_sums[:], scalar1=REDUCTION, scalar2=-CLAMP, op0=ALU.mult, op1=ALU.max
         )
-        nc.vector.tensor_scalar_min(out=logits[:], in0=logits[:], scalar1=CLAMP)
-
-        halves = keep.tile([P, IMAGES, CLASSES], F32)
-        nc.vector.tensor_tensor(out=halves[:], in0=logits[:, :, 0, :], in1=logits[:, :, 1, :], op=ALU.add)
-        mean_ps = turned_psum.tile([P, CHANNELS], F32, tag="turned_ps")
-        nc.tensor.matmul(
-            out=mean_ps[:, 0 : IMAGES * CLASSES], lhsT=ones[:], rhs=halves[:].rearrange("p b k -> p (b k)"),
-            start=True, stop=True,
-        )
 
         group_shape = [P, IMAGES, PIXEL_TILES, CLASSES]
         top = keep.tile([P, IMAGES, PIXEL_TILES], F32)
@@ -284,6 +320,13 @@ def tile_cssrclassifier_pa_e_kernel(tc, d, W_dec_words, W_dec_scales, x, out_0, 
         )
         expd = keep.tile(group_shape, F32)
         nc.scalar.activation(out=expd[:], in_=shifted[:], func=ACT.Exp)
+        halves = keep.tile([P, IMAGES, CLASSES], F32)
+        nc.vector.tensor_tensor(out=halves[:], in0=logits[:, :, 0, :], in1=logits[:, :, 1, :], op=ALU.add)
+        mean_ps = turned_psum.tile([P, CHANNELS], F32, tag="turned_ps")
+        nc.tensor.matmul(
+            out=mean_ps[:, 0 : IMAGES * CLASSES], lhsT=ones[:], rhs=halves[:].rearrange("p b k -> p (b k)"),
+            start=True, stop=True,
+        )
         mean_sb = keep.tile([P, CLASSES], F32)
         for b in range(IMAGES):
             nc.scalar.mul(

@@ -25,7 +25,7 @@ ROUNDS = CLASSES * IMAGES // PAIR
 C_TILES = CHANNELS // P
 PIXEL_TILES = PIXELS // P
 PLANES_PER_TILE = 4
-LOADS_AHEAD = 6
+CLASSES_AHEAD = 4
 REGROUP_AHEAD = 3
 FIRST_PIXELS = 176
 REDUCTION = -0.1
@@ -39,7 +39,7 @@ def tile_cssrclassifier_pa_e_kernel(tc, d, W_dec_words, W_dec_scales, x, out_0, 
     with ExitStack() as ctx:
         ctx.enter_context(tc.manual_schedule())
         keep = ctx.enter_context(tc.tile_pool(name="keep", bufs=1))
-        raw_pool = ctx.enter_context(tc.tile_pool(name="raw", bufs=LOADS_AHEAD))
+        raw_pool = ctx.enter_context(tc.tile_pool(name="raw", bufs=CLASSES_AHEAD))
         grouped_pool = ctx.enter_context(tc.tile_pool(name="grouped", bufs=2))
         quant_pool = ctx.enter_context(tc.tile_pool(name="quant", bufs=3))
         recon_pool = ctx.enter_context(tc.tile_pool(name="recon", bufs=6))
@@ -74,21 +74,24 @@ def tile_cssrclassifier_pa_e_kernel(tc, d, W_dec_words, W_dec_scales, x, out_0, 
         nc.gpsimd.memset(recon_sums[:], 0.0)
         nc.gpsimd.memset(x_sums[:], 0.0)
 
+        d_class = {}
         d_raw = {}
         d_grouped = {}
         d_codes = {}
         d_scales = {}
 
-        def load(j):
-            k, pair = divmod(j, IMAGES // PAIR)
-            raw = raw_pool.tile([P, PAIR, PACK * PIXELS], BF16)
+        def load_d(k, first, count):
+            if first == 0:
+                raw = raw_pool.tile([P, IMAGES, PACK * PIXELS], BF16)
+                d_class[k] = raw
+                for pair in range(IMAGES // PAIR):
+                    d_raw[(IMAGES // PAIR) * k + pair] = raw[:, PAIR * pair : PAIR * (pair + 1), :]
             nc.sync.dma_start(
-                out=raw[:],
-                in_=d[k, PAIR * pair : PAIR * (pair + 1)].rearrange("b (p t) h w -> p b (t h w)", t=PACK),
+                out=d_class[k][:, first : first + count, :],
+                in_=d[k, first : first + count].rearrange("b (p t) h w -> p b (t h w)", t=PACK),
             )
-            d_raw[j] = raw
-            if pair != 0:
-                return
+
+        def load_w(k):
             if k % PLANES_PER_TILE == 0:
                 group = k // PLANES_PER_TILE
                 for quadrant in range(4):
@@ -146,7 +149,7 @@ def tile_cssrclassifier_pa_e_kernel(tc, d, W_dec_words, W_dec_scales, x, out_0, 
             d_grouped[j] = grouped
             engine.tensor_scalar(
                 out=grouped[:, :, 0:last, :],
-                in0=d_raw[j][:].rearrange("p b (t w) -> p b w t", t=PACK)[:, :, 0:last, :],
+                in0=d_raw[j].rearrange("p b (t w) -> p b w t", t=PACK)[:, :, 0:last, :],
                 scalar1=1.0,
                 scalar2=0.0,
                 op0=ALU.mult,
@@ -156,7 +159,7 @@ def tile_cssrclassifier_pa_e_kernel(tc, d, W_dec_words, W_dec_scales, x, out_0, 
         def regroup_scalar(j, first, last):
             nc.scalar.copy(
                 out=d_grouped[j][:, :, first:last, :],
-                in_=d_raw[j][:].rearrange("p b (t w) -> p b w t", t=PACK)[:, :, first:last, :],
+                in_=d_raw[j].rearrange("p b (t w) -> p b w t", t=PACK)[:, :, first:last, :],
             )
 
         def quantise(j):
@@ -260,19 +263,22 @@ def tile_cssrclassifier_pa_e_kernel(tc, d, W_dec_words, W_dec_scales, x, out_0, 
                     recon_way(i)
                     turned_way(i)
                 scalar_sums()
-            for b2 in range(PAIR):
-                nc.sync.dma_start(
-                    out=out_2[PAIR * pair + b2, k].rearrange("(p ct) h w -> p (ct h w)", p=P),
-                    in_=recon[:, b2, :, :].rearrange("p ct w -> p (ct w)"),
-                )
+            nc.sync.dma_start(
+                out=out_2[PAIR * pair : PAIR * (pair + 1), k].rearrange("b (p ct) h w -> p b (ct h w)", p=P),
+                in_=recon[:].rearrange("p b ct w -> p b (ct w)"),
+            )
 
-        load(0)
+        load_d(0, 0, PAIR)
+        load_w(0)
         load_x(0)
-        load(1)
-        load(2)
+        load_d(0, PAIR, PAIR)
+        load_d(1, 0, PAIR)
+        load_w(1)
         load_x(1)
-        for j in range(3, LOADS_AHEAD):
-            load(j)
+        load_d(1, PAIR, PAIR)
+        for k in range(2, CLASSES_AHEAD):
+            load_d(k, 0, IMAGES)
+            load_w(k)
         regroup_first(0, nc.vector, FIRST_PIXELS)
         regroup_scalar(0, FIRST_PIXELS, PIXELS)
         permute_planes(0, nc.vector)
@@ -282,8 +288,9 @@ def tile_cssrclassifier_pa_e_kernel(tc, d, W_dec_words, W_dec_scales, x, out_0, 
         regroup_scalar(1, FIRST_PIXELS, PIXELS)
         turn_x(0)
         for j in range(ROUNDS):
-            if j + LOADS_AHEAD < ROUNDS:
-                load(j + LOADS_AHEAD)
+            if j % (IMAGES // PAIR) == 0 and j // (IMAGES // PAIR) + CLASSES_AHEAD < CLASSES:
+                load_d(j // (IMAGES // PAIR) + CLASSES_AHEAD, 0, IMAGES)
+                load_w(j // (IMAGES // PAIR) + CLASSES_AHEAD)
             if j + 1 < ROUNDS:
                 quantise(j + 1)
             multiply(j)

@@ -28,6 +28,7 @@ PLANES_PER_TILE = 4
 CLASSES_AHEAD = 4
 REGROUP_AHEAD = 3
 FIRST_PIXELS = 176
+GPSIMD_PIXELS = 192
 REDUCTION = -0.1
 CLAMP = 500.0
 
@@ -64,7 +65,7 @@ def tile_cssrclassifier_pa_e_kernel(tc, d, W_dec_words, W_dec_scales, x, out_0, 
         x_sums = keep.tile([P, IMAGES, PIXEL_TILES], F32)
         warm = keep.tile([P, 2], F32)
 
-        nc.vector.memset(w_planes_raw[:].bitcast(I32), 0)
+        nc.gpsimd.memset(w_planes_raw[:].bitcast(F32), 0.0)
         nc.vector.memset(warm[:], 0.0)
         nc.scalar.activation(out=warm[:, 1:2], in_=warm[:, 0:1], func=ACT.Exp)
         make_identity(nc, ident_bf[:])
@@ -91,14 +92,15 @@ def tile_cssrclassifier_pa_e_kernel(tc, d, W_dec_words, W_dec_scales, x, out_0, 
                 in_=d[k, first : first + count].rearrange("b (p t) h w -> p b (t h w)", t=PACK),
             )
 
+        def load_planes(group):
+            k = PLANES_PER_TILE * group
+            for quadrant in range(4):
+                nc.sync.dma_start(
+                    out=w_planes_raw[32 * quadrant : 32 * quadrant + 16, group, :].bitcast(I32),
+                    in_=W_dec_scales[k : k + PLANES_PER_TILE, 4 * quadrant : 4 * quadrant + 4, :].bitcast(I32),
+                )
+
         def load_w(k):
-            if k % PLANES_PER_TILE == 0:
-                group = k // PLANES_PER_TILE
-                for quadrant in range(4):
-                    nc.sync.dma_start(
-                        out=w_planes_raw[32 * quadrant : 32 * quadrant + 16, group, :].bitcast(I32),
-                        in_=W_dec_scales[k : k + PLANES_PER_TILE, 4 * quadrant : 4 * quadrant + 4, :].bitcast(I32),
-                    )
             nc.sync.dma_start(
                 out=w_codes_raw[:, k, :].bitcast(I32),
                 in_=W_dec_words[k].rearrange("p n t -> p (n t)").bitcast(I32),
@@ -154,6 +156,12 @@ def tile_cssrclassifier_pa_e_kernel(tc, d, W_dec_words, W_dec_scales, x, out_0, 
                 scalar2=0.0,
                 op0=ALU.mult,
                 op1=ALU.add,
+            )
+
+        def regroup_vector(j, first, last):
+            nc.vector.tensor_copy(
+                out=d_grouped[j][:, :, first:last, :],
+                in_=d_raw[j].rearrange("p b (t w) -> p b w t", t=PACK)[:, :, first:last, :],
             )
 
         def regroup_scalar(j, first, last):
@@ -268,9 +276,11 @@ def tile_cssrclassifier_pa_e_kernel(tc, d, W_dec_words, W_dec_scales, x, out_0, 
                 in_=recon[:].rearrange("p b ct w -> p b (ct w)"),
             )
 
-        load_d(0, 0, PAIR)
+        load_planes(0)
         load_w(0)
+        load_d(0, 0, PAIR)
         load_x(0)
+        load_planes(1)
         load_d(0, PAIR, PAIR)
         load_d(1, 0, PAIR)
         load_w(1)
@@ -279,10 +289,11 @@ def tile_cssrclassifier_pa_e_kernel(tc, d, W_dec_words, W_dec_scales, x, out_0, 
         for k in range(2, CLASSES_AHEAD):
             load_d(k, 0, IMAGES)
             load_w(k)
-        regroup_first(0, nc.vector, FIRST_PIXELS)
-        regroup_scalar(0, FIRST_PIXELS, PIXELS)
         permute_planes(0, nc.vector)
         permute_codes(0, nc.vector)
+        permute_planes(1, nc.gpsimd)
+        regroup_first(0, nc.vector, FIRST_PIXELS)
+        regroup_scalar(0, FIRST_PIXELS, PIXELS)
         quantise(0)
         regroup_first(1, nc.vector, FIRST_PIXELS)
         regroup_scalar(1, FIRST_PIXELS, PIXELS)
@@ -297,11 +308,10 @@ def tile_cssrclassifier_pa_e_kernel(tc, d, W_dec_words, W_dec_scales, x, out_0, 
             if j == 0:
                 turn_x(1)
             for r in range(REGROUP_AHEAD - 1 if j == 0 else j + REGROUP_AHEAD, min(j + REGROUP_AHEAD + 1, ROUNDS)):
-                regroup_first(r, nc.gpsimd, PIXELS)
+                regroup_first(r, nc.gpsimd, GPSIMD_PIXELS)
+                regroup_vector(r, GPSIMD_PIXELS, PIXELS)
             if j % (IMAGES // PAIR) == 0 and j // (IMAGES // PAIR) + 1 < CLASSES:
                 permute_codes(j // (IMAGES // PAIR) + 1, nc.gpsimd)
-            if j == PLANES_PER_TILE:
-                permute_planes(1, nc.gpsimd)
 
         abs_sums = keep.tile([P, IMAGES, PIXEL_TILES, CLASSES], F32)
         nc.vector.scalar_tensor_tensor(

from contextlib import ExitStack

import concourse.mybir as mybir
from concourse.masks import make_identity

F32 = mybir.dt.float32
BF16 = mybir.dt.bfloat16
I32 = mybir.dt.int32
U32 = mybir.dt.uint32
U8 = mybir.dt.uint8
FP8X4 = mybir.dt.float8_e4m3fn_x4
ALU = mybir.AluOpType
ACT = mybir.ActivationFunctionType
AXIS = mybir.AxisListType

P = 128
PACK = 4
CLASSES = 8
IMAGES = 4
CHANNELS = 512
HIDDEN = 512
PIXELS = 256
PAIR = 2
ROUNDS = CLASSES * IMAGES // PAIR
C_TILES = CHANNELS // P
PIXEL_TILES = PIXELS // P
PLANES_PER_TILE = 4
CLASSES_AHEAD = 4
REGROUP_AHEAD = 3
FIRST_PIXELS = 176
GPSIMD_PIXELS = 192
REDUCTION = -0.1
CLAMP = 500.0

FLOPS = 2 * CLASSES * IMAGES * CHANNELS * HIDDEN * PIXELS


def tile_cssrclassifier_pa_e_kernel(tc, d, W_dec_words, W_dec_scales, x, out_0, out_1, out_2):
    nc = tc.nc
    with ExitStack() as ctx:
        ctx.enter_context(tc.manual_schedule())
        keep = ctx.enter_context(tc.tile_pool(name="keep", bufs=1))
        raw_pool = ctx.enter_context(tc.tile_pool(name="raw", bufs=CLASSES_AHEAD))
        grouped_pool = ctx.enter_context(tc.tile_pool(name="grouped", bufs=2))
        quant_pool = ctx.enter_context(tc.tile_pool(name="quant", bufs=3))
        recon_pool = ctx.enter_context(tc.tile_pool(name="recon", bufs=6))
        diff_pool = ctx.enter_context(tc.tile_pool(name="diff", bufs=3))
        unread_pool = ctx.enter_context(tc.tile_pool(name="unread", bufs=2))
        recon_psum = ctx.enter_context(tc.psum_pool(name="recon_psum", bufs=3))
        turned_psum = ctx.enter_context(tc.psum_pool(name="turned_psum", bufs=3))
        folded_psum = ctx.enter_context(tc.psum_pool(name="folded_psum", bufs=2))

        w_codes_raw = keep.tile([P, CLASSES, CHANNELS], U32)
        w_planes_raw = keep.tile([P, CLASSES // PLANES_PER_TILE, CHANNELS], U8)
        w_codes = keep.tile([P, CLASSES, CHANNELS], U32, align_bytes=64)
        w_planes = keep.tile([P, CLASSES // PLANES_PER_TILE, CHANNELS], U8, align_bytes=64)
        x_raw = keep.tile([P, IMAGES, C_TILES, PIXELS], BF16)
        x_turned = keep.tile([P, IMAGES, PIXEL_TILES, CHANNELS], BF16)
        ident = keep.tile([P, P], F32)
        ident_bf = keep.tile([P, P], BF16)
        ones = keep.tile([P, P], F32)
        prob_cols = keep.tile([P, P], F32)
        max_sums = keep.tile([P, IMAGES, PIXEL_TILES, CLASSES], F32)
        recon_sums = keep.tile([P, IMAGES, PIXEL_TILES, CLASSES], F32)
        x_sums = keep.tile([P, IMAGES, PIXEL_TILES], F32)
        warm = keep.tile([P, 2], F32)

        nc.gpsimd.memset(w_planes_raw[:].bitcast(F32), 0.0)
        nc.vector.memset(warm[:], 0.0)
        nc.scalar.activation(out=warm[:, 1:2], in_=warm[:, 0:1], func=ACT.Exp)
        make_identity(nc, ident_bf[:])
        make_identity(nc, ident[:])
        nc.gpsimd.memset(ones[:], 1.0)
        nc.gpsimd.memset(prob_cols[:], 0.0)
        nc.gpsimd.memset(recon_sums[:], 0.0)
        nc.gpsimd.memset(x_sums[:], 0.0)

        d_class = {}
        d_raw = {}
        d_grouped = {}
        d_codes = {}
        d_scales = {}

        def load_d(k, first, count):
            if first == 0:
                raw = raw_pool.tile([P, IMAGES, PACK * PIXELS], BF16)
                d_class[k] = raw
                for pair in range(IMAGES // PAIR):
                    d_raw[(IMAGES // PAIR) * k + pair] = raw[:, PAIR * pair : PAIR * (pair + 1), :]
            nc.sync.dma_start(
                out=d_class[k][:, first : first + count, :],
                in_=d[k, first : first + count].rearrange("b (p t) h w -> p b (t h w)", t=PACK),
            )

        def load_planes(group):
            k = PLANES_PER_TILE * group
            for quadrant in range(4):
                nc.sync.dma_start(
                    out=w_planes_raw[32 * quadrant : 32 * quadrant + 16, group, :].bitcast(I32),
                    in_=W_dec_scales[k : k + PLANES_PER_TILE, 4 * quadrant : 4 * quadrant + 4, :].bitcast(I32),
                )

        def load_w(k):
            nc.sync.dma_start(
                out=w_codes_raw[:, k, :].bitcast(I32),
                in_=W_dec_words[k].rearrange("p n t -> p (n t)").bitcast(I32),
            )

        def load_x(pair):
            images = slice(PAIR * pair, PAIR * (pair + 1))
            nc.sync.dma_start(
                out=x_raw[:, images].rearrange("p b ct w -> p b (ct w)"),
                in_=x[images].rearrange("b (p ct) h w -> p b (ct h w)", p=P),
            )

        def permute_codes(k, engine):
            engine.tensor_copy(
                out=w_codes[:, k, :].bitcast(I32).rearrange("p (ct m) -> p ct m", ct=C_TILES),
                in_=w_codes_raw[:, k, :].bitcast(I32).rearrange("p (m ct) -> p ct m", ct=C_TILES),
            )

        def permute_planes(group, engine):
            engine.tensor_copy(
                out=w_planes[:, group, :].rearrange("p (ct m) -> p m ct", ct=C_TILES),
                in_=w_planes_raw[:, group, :].rearrange("p (m ct) -> p m ct", ct=C_TILES),
            )

        def direct(pair, i):
            return i <= pair

        def turn_x(pair):
            for b in range(PAIR * pair, PAIR * (pair + 1)):
                for half in range(PIXEL_TILES):
                    pixels = slice(half * P, (half + 1) * P)
                    turned_ps = turned_psum.tile([P, CHANNELS], F32)
                    as_bf16 = turned_ps[:].bitcast(BF16)
                    for ct in range(C_TILES):
                        nc.tensor.transpose(
                            out=as_bf16[:, ct * P : (ct + 1) * P], in_=x_raw[:, b, ct, pixels], identity=ident_bf[:]
                        )
                    if direct(pair, PIXEL_TILES * (b - PAIR * pair) + half):
                        nc.scalar.copy(out=x_turned[:, b, half, :], in_=as_bf16[:, 0:CHANNELS])
                    else:
                        nc.scalar.activation(
                            out=x_turned[:, b, half, :], in_=as_bf16[:, 0:CHANNELS], func=ACT.Copy,
                            accum_out=x_sums[:, b, half : half + 1],
                        )

        def regroup_first(j, engine, last):
            grouped = grouped_pool.tile([P, PAIR, PIXELS, PACK], BF16, align_bytes=64)
            d_grouped[j] = grouped
            engine.tensor_scalar(
                out=grouped[:, :, 0:last, :],
                in0=d_raw[j].rearrange("p b (t w) -> p b w t", t=PACK)[:, :, 0:last, :],
                scalar1=1.0,
                scalar2=0.0,
                op0=ALU.mult,
                op1=ALU.add,
            )

        def regroup_vector(j, first, last):
            nc.vector.tensor_copy(
                out=d_grouped[j][:, :, first:last, :],
                in_=d_raw[j].rearrange("p b (t w) -> p b w t", t=PACK)[:, :, first:last, :],
            )

        def regroup_scalar(j, first, last):
            nc.scalar.copy(
                out=d_grouped[j][:, :, first:last, :],
                in_=d_raw[j].rearrange("p b (t w) -> p b w t", t=PACK)[:, :, first:last, :],
            )

        def quantise(j):
            codes = quant_pool.tile([P, PAIR * PIXELS], U32, align_bytes=64)
            scales = quant_pool.tile([P, PAIR * PIXELS], U8, align_bytes=64)
            nc.vector.quantize_mx(
                out=codes[:].bitcast(FP8X4),
                scales=scales[:],
                in_=d_grouped[j][:].rearrange("p b w t -> p (b w t)"),
            )
            d_codes[j] = codes
            d_scales[j] = scales

        def multiply(j):
            k, pair = divmod(j, IMAGES // PAIR)
            offset = 4 * (k % PLANES_PER_TILE)
            group = k // PLANES_PER_TILE
            last_round = j == ROUNDS - 1
            recon = recon_pool.tile([P, PAIR, C_TILES, PIXELS], F32)
            folded_ps = folded_psum.tile([P, PAIR * PIXEL_TILES, P], F32)
            diffs = {}

            def recon_way(i):
                cols = slice(i * P, (i + 1) * P)
                recon_ps = recon_psum.tile([P, PAIR * PIXELS], F32)
                nc.tensor.matmul_mx(
                    out=recon_ps[:],
                    lhsT=w_codes[:, k, cols].bitcast(FP8X4),
                    lhsT_scale=w_planes[offset:P, group, cols],
                    rhs=d_codes[j][:].bitcast(FP8X4),
                    rhs_scale=d_scales[j][:],
                    start=True,
                    stop=True,
                )
                if pair == 1 and i == C_TILES - 1 and not last_round:
                    nc.vector.tensor_copy(out=recon[:, :, i, :], in_=recon_ps[:].rearrange("p (b w) -> p b w", b=PAIR))
                else:
                    nc.scalar.copy(out=recon[:, :, i, :], in_=recon_ps[:].rearrange("p (b w) -> p b w", b=PAIR))

            def turned_way(i):
                cols = slice(i * P, (i + 1) * P)
                b2, half = divmod(i, PIXEL_TILES)
                b = PAIR * pair + b2
                turned_ps = turned_psum.tile([P, CHANNELS], F32)
                nc.tensor.matmul_mx(
                    out=turned_ps[:],
                    lhsT=d_codes[j][:, cols].bitcast(FP8X4),
                    lhsT_scale=d_scales[j][:, cols],
                    rhs=w_codes[:, k, :].bitcast(FP8X4),
                    rhs_scale=w_planes[offset:P, group, :],
                    start=True,
                    stop=True,
                )
                if direct(pair, i):
                    diff = diff_pool.tile([P, CHANNELS], F32)
                    nc.vector.tensor_tensor(
                        out=diff[:], in0=turned_ps[:], in1=x_turned[:, b, half, :], op=ALU.subtract
                    )
                    diffs[i] = diff
                else:
                    unread = unread_pool.tile([P, CHANNELS], F32)
                    nc.vector.scalar_tensor_tensor(
                        out=unread[:], in0=turned_ps[:], scalar=1.0, in1=x_turned[:, b, half, :],
                        op0=ALU.mult, op1=ALU.max, accum_out=max_sums[:, b, half, k : k + 1],
                    )
                    for ct in range(C_TILES):
                        nc.tensor.matmul_mx(
                            out=folded_ps[:, i, :],
                            lhsT=d_codes[j][:, cols].bitcast(FP8X4),
                            lhsT_scale=d_scales[j][:, cols],
                            rhs=w_codes[:, k, ct * P : (ct + 1) * P].bitcast(FP8X4),
                            rhs_scale=w_planes[offset:P, group, ct * P : (ct + 1) * P],
                            start=(ct == 0),
                            stop=(ct == C_TILES - 1),
                        )

            def scalar_sums():
                for i in range(PAIR * PIXEL_TILES):
                    b2, half = divmod(i, PIXEL_TILES)
                    if direct(pair, i):
                        unread_d = unread_pool.tile([P, CHANNELS], BF16)
                        nc.scalar.activation(
                            out=unread_d[:], in_=diffs[i][:], func=ACT.Abs, scale=0.5,
                            accum_out=max_sums[:, PAIR * pair + b2, half, k : k + 1],
                        )
                    else:
                        unread_s = unread_pool.tile([P, P], BF16)
                        nc.scalar.activation(
                            out=unread_s[:], in_=folded_ps[:, i, :], func=ACT.Copy,
                            accum_out=recon_sums[:, PAIR * pair + b2, half, k : k + 1],
                        )

            if last_round:
                for i in range(C_TILES):
                    turned_way(i)
                scalar_sums()
                for i in range(C_TILES):
                    recon_way(i)
            else:
                for i in range(C_TILES):
                    recon_way(i)
                    turned_way(i)
                scalar_sums()
            nc.sync.dma_start(
                out=out_2[PAIR * pair : PAIR * (pair + 1), k].rearrange("b (p ct) h w -> p b (ct h w)", p=P),
                in_=recon[:].rearrange("p b ct w -> p b (ct w)"),
            )

        load_planes(0)
        load_w(0)
        load_d(0, 0, PAIR)
        load_x(0)
        load_planes(1)
        load_d(0, PAIR, PAIR)
        load_d(1, 0, PAIR)
        load_w(1)
        load_x(1)
        load_d(1, PAIR, PAIR)
        for k in range(2, CLASSES_AHEAD):
            load_d(k, 0, IMAGES)
            load_w(k)
        permute_planes(0, nc.vector)
        permute_codes(0, nc.vector)
        permute_planes(1, nc.gpsimd)
        regroup_first(0, nc.vector, FIRST_PIXELS)
        regroup_scalar(0, FIRST_PIXELS, PIXELS)
        quantise(0)
        regroup_first(1, nc.vector, FIRST_PIXELS)
        regroup_scalar(1, FIRST_PIXELS, PIXELS)
        turn_x(0)
        for j in range(ROUNDS):
            if j % (IMAGES // PAIR) == 0 and j // (IMAGES // PAIR) + CLASSES_AHEAD < CLASSES:
                load_d(j // (IMAGES // PAIR) + CLASSES_AHEAD, 0, IMAGES)
                load_w(j // (IMAGES // PAIR) + CLASSES_AHEAD)
            if j + 1 < ROUNDS:
                quantise(j + 1)
            multiply(j)
            if j == 0:
                turn_x(1)
            for r in range(REGROUP_AHEAD - 1 if j == 0 else j + REGROUP_AHEAD, min(j + REGROUP_AHEAD + 1, ROUNDS)):
                regroup_first(r, nc.gpsimd, GPSIMD_PIXELS)
                regroup_vector(r, GPSIMD_PIXELS, PIXELS)
            if j % (IMAGES // PAIR) == 0 and j // (IMAGES // PAIR) + 1 < CLASSES:
                permute_codes(j // (IMAGES // PAIR) + 1, nc.gpsimd)

        abs_sums = keep.tile([P, IMAGES, PIXEL_TILES, CLASSES], F32)
        nc.vector.scalar_tensor_tensor(
            out=abs_sums[:].rearrange("p b s k -> p (b s k)"), in0=max_sums[:].rearrange("p b s k -> p (b s k)"),
            scalar=2.0, in1=recon_sums[:].rearrange("p b s k -> p (b s k)"), op0=ALU.mult, op1=ALU.subtract,
        )
        nc.vector.tensor_tensor(
            out=abs_sums[:], in0=abs_sums[:],
            in1=x_sums[:].unsqueeze(3).to_broadcast([P, IMAGES, PIXEL_TILES, CLASSES]), op=ALU.subtract,
        )

        logits = keep.tile([P, IMAGES, PIXEL_TILES, CLASSES], F32)
        nc.vector.tensor_scalar(
            out=logits[:], in0=abs_sums[:], scalar1=REDUCTION, scalar2=-CLAMP, op0=ALU.mult, op1=ALU.max
        )

        group_shape = [P, IMAGES, PIXEL_TILES, CLASSES]
        top = keep.tile([P, IMAGES, PIXEL_TILES], F32)
        nc.vector.tensor_reduce(out=top[:], in_=logits[:], axis=AXIS.X, op=ALU.max)
        shifted = keep.tile(group_shape, F32)
        nc.vector.tensor_tensor(
            out=shifted[:], in0=logits[:], in1=top[:].unsqueeze(3).to_broadcast(group_shape), op=ALU.subtract
        )
        expd = keep.tile(group_shape, F32)
        nc.scalar.activation(out=expd[:], in_=shifted[:], func=ACT.Exp)
        halves = keep.tile([P, IMAGES, CLASSES], F32)
        nc.vector.tensor_tensor(out=halves[:], in0=logits[:, :, 0, :], in1=logits[:, :, 1, :], op=ALU.add)
        mean_ps = turned_psum.tile([P, CHANNELS], F32, tag="turned_ps")
        nc.tensor.matmul(
            out=mean_ps[:, 0 : IMAGES * CLASSES], lhsT=ones[:], rhs=halves[:].rearrange("p b k -> p (b k)"),
            start=True, stop=True,
        )
        mean_sb = keep.tile([P, CLASSES], F32)
        for b in range(IMAGES):
            nc.scalar.mul(
                out=mean_sb[32 * b : 32 * b + 1, :],
                in_=mean_ps[32 * b : 32 * b + 1, b * CLASSES : (b + 1) * CLASSES],
                mul=1.0 / PIXELS,
            )
        nc.sync.dma_start(out=out_1, in_=mean_sb[0:P:32, :])
        total = keep.tile([P, IMAGES, PIXEL_TILES], F32)
        nc.vector.tensor_reduce(out=total[:], in_=expd[:], axis=AXIS.X, op=ALU.add)
        inverse = keep.tile([P, IMAGES, PIXEL_TILES], F32)
        nc.vector.reciprocal(out=inverse[:], in_=total[:])
        nc.vector.tensor_tensor(
            out=prob_cols[:, 0 : IMAGES * CLASSES * PIXEL_TILES].rearrange(
                "p (b k s) -> p b s k", b=IMAGES, k=CLASSES
            ),
            in0=expd[:],
            in1=inverse[:].unsqueeze(3).to_broadcast(group_shape),
            op=ALU.mult,
        )
        prob_ps = turned_psum.tile([P, CHANNELS], F32, tag="turned_ps")
        nc.tensor.transpose(out=prob_ps[:, 0:P], in_=prob_cols[:], identity=ident[:])
        prob_rows = keep.tile([P, P], F32)
        nc.vector.tensor_copy(out=prob_rows[:], in_=prob_ps[:, 0:P])
        nc.sync.dma_start(
            out=out_0.rearrange("b k (s h) w -> (b k s) (h w)", s=PIXEL_TILES),
            in_=prob_rows[0 : IMAGES * CLASSES * PIXEL_TILES, :],
        )
